import numpy as np
import ml_dtypes


def mxq(x, axis, fmt="e4m3"):
    dtype, down = {"e4m3": (ml_dtypes.float8_e4m3fn, 7), "e5m2": (ml_dtypes.float8_e5m2, 14)}[fmt]
    v = np.moveaxis(np.asarray(x, np.float32).astype(ml_dtypes.bfloat16).astype(np.float64), axis, -1)
    blocks = v.reshape(v.shape[:-1] + (-1, 32))
    amax = np.abs(blocks).max(-1, keepdims=True)
    byte = np.maximum(np.where(amax > 0, np.frexp(amax)[1] - 1 + 127, 0) - down, 1)
    scale = np.exp2(byte - 127.0)
    codes = (blocks / scale).astype(np.float32).astype(dtype).astype(np.float64)
    return np.moveaxis((codes * scale).reshape(v.shape), -1, axis)


WIDE = False


def mx_kscale(k):
    if not WIDE:
        return np.ones(k)
    levels = np.array([10, -10, 5, -5, 0])
    a = np.random.permutation(np.resize(levels, k // 512 * 4)).reshape(k // 512, 4)
    idx = np.arange(k)
    return np.exp2(a[idx // 512, idx % 128 // 32])


BF16 = ml_dtypes.bfloat16


def bf(x):
    return np.asarray(x, np.float32).astype(BF16)


def f64(x):
    return np.asarray(x).astype(np.float64)


E2M1 = np.array([0.0, 0.5, 1.0, 1.5, 2.0, 3.0, 4.0, 6.0, -0.0, -0.5, -1.0, -1.5, -2.0, -3.0, -4.0, -6.0])


def pack_weight(w, fmt):
    k, n = w.shape
    w = f64(bf(w)).reshape(k // 32, 32, n)
    amax = np.abs(w).max(1)
    if fmt == "e4m3":
        byte = np.frexp(amax)[1] - 1 + 127 - 7
    else:
        mant, ex = np.frexp(amax / 6.0)
        byte = np.where(mant > 0.5, ex, ex - 1) + 127
    byte = np.clip(np.where(amax > 0, byte, 1), 1, 254)
    scaled = (w * np.exp2(127.0 - byte)[:, None, :]).reshape(k, n).astype(np.float32)
    by_word = np.ascontiguousarray(scaled.reshape(k // 512, 128, 4, n).transpose(0, 1, 3, 2))
    if fmt == "e4m3":
        words = by_word.astype(ml_dtypes.float8_e4m3fn).view(np.uint8)
    else:
        c = by_word.astype(ml_dtypes.float4_e2m1fn).view(np.uint8) & 0xF
        words = c[..., 0::2] | (c[..., 1::2] << 4)
    return np.ascontiguousarray(words), np.ascontiguousarray(byte.astype(np.uint8).reshape(k // 512, 16, n))


def unpack_weight(words, scales, fmt):
    g, p, n, _ = words.shape
    if fmt == "e4m3":
        vals = np.ascontiguousarray(words).view(ml_dtypes.float8_e4m3fn).astype(np.float64)
    else:
        nib = np.empty((g, p, n, 4), np.uint8)
        nib[..., 0::2] = words & 0xF
        nib[..., 1::2] = words >> 4
        vals = E2M1[nib]
    vals = vals * np.repeat(np.exp2(scales.astype(np.float64) - 127.0), 8, axis=1)[..., None]
    return vals.transpose(0, 1, 3, 2).reshape(g * 512, n)

def pack4(w):
    words, scales = pack_weight(w, "e2m1")
    return words.reshape(words.shape[0], 128, -1), scales


def unpack4(words, scales):
    return unpack_weight(words.reshape(words.shape[0], 128, -1, 2), scales, "e2m1")


B, S, H, HD = 2, 128, 8, 64
D = H * HD
HALF = HD // 2


def apply_rope(t, cos, sin):
    t0 = t[..., 0::2]
    t1 = t[..., 1::2]
    out0 = t0 * cos - t1 * sin
    out1 = t0 * sin + t1 * cos
    return np.stack([out0, out1], axis=-1).reshape(t.shape)


def setup_inputs():
    s = mx_kscale(D)
    phi = np.random.uniform(0.0, 2.0 * np.pi, (S, HALF))
    x = bf(np.random.standard_normal((B, S, D)) * s)
    words, scales = pack4(np.random.standard_normal((D, 3 * D)) / np.sqrt(D) / s[:, None])
    return {"x": x,
            "w_qkv_words": words, "w_qkv_scales": scales,
            "cos": bf(np.cos(phi)), "sin": bf(np.sin(phi))}


def reference(x, w_qkv_words, w_qkv_scales, cos, sin):
    qkv = mxq(f64(x), 2, "e4m3") @ unpack4(w_qkv_words, w_qkv_scales)
    qkv = qkv.reshape(B, S, 3, H, HD).transpose(2, 0, 3, 1, 4)
    q, k, v = qkv[0], qkv[1], qkv[2]
    c, sn = f64(cos), f64(sin)
    return apply_rope(q, c, sn), apply_rope(k, c, sn), np.ascontiguousarray(v)

@@ -1,0 +1,159 @@
+import concourse.mybir as mybir
+from concourse.masks import make_identity
+
+F32 = mybir.dt.float32
+BF16 = mybir.dt.bfloat16
+I32 = mybir.dt.int32
+U8 = mybir.dt.uint8
+U32 = mybir.dt.uint32
+FP8X4 = mybir.dt.float8_e4m3fn_x4
+FP4X4 = mybir.dt.float4_e2m1fn_x4
+MULT = mybir.AluOpType.mult
+ADD = mybir.AluOpType.add
+
+P = 128
+BATCH = 2
+SEQ = 128
+HEADS = 8
+HEAD_DIM = 64
+PAIRS = HEAD_DIM // 2
+MODEL = HEADS * HEAD_DIM
+PACK = 4
+PARITY = 2
+ROWS = SEQ // PARITY
+UNIT_HEADS = 4
+UNIT_COLS = UNIT_HEADS * HEAD_DIM
+
+FLOPS = 2 * BATCH * SEQ * MODEL * 3 * MODEL
+
+
+def tile_ropeflashattention_pa_s_kernel(
+    tc, x, w_qkv_words, w_qkv_scales, cos, sin, out_0, out_1, out_2
+):
+    nc = tc.nc
+    outputs = (out_0, out_1, out_2)
+
+    with tc.tile_pool(name="keep", bufs=1) as keep, tc.tile_pool(
+        name="work", bufs=4
+    ) as work, tc.tile_pool(name="results", bufs=6) as results, tc.psum_pool(
+        name="turned", bufs=2
+    ) as turned, tc.psum_pool(name="sums", bufs=6) as sums:
+        x_sb = keep.tile([P, PARITY * MODEL], BF16)
+        nc.sync.dma_start(
+            out=x_sb[:], in_=x.rearrange("b (i e) k -> i b (e k)", e=PARITY)
+        )
+
+        w_scales = keep.tile([P, 3 * MODEL], U8, align_bytes=64)
+        nc.vector.memset(w_scales[:].bitcast(I32), 0)
+        for quadrant in range(4):
+            nc.sync.dma_start(
+                out=w_scales[32 * quadrant : 32 * quadrant + 4, :].bitcast(I32),
+                in_=w_qkv_scales[0, 4 * quadrant : 4 * quadrant + 4, :].bitcast(I32),
+            )
+
+        w_words = keep.tile([P, 2 * 3 * MODEL], U8, align_bytes=64)
+        nc.sync.dma_start(out=w_words[:].bitcast(I32), in_=w_qkv_words[0].bitcast(I32))
+
+        cos_sb = keep.tile([P, PARITY * PAIRS], BF16)
+        sin_sb = keep.tile([P, PARITY * PAIRS], BF16)
+        for table_sb, table in ((cos_sb, cos), (sin_sb, sin)):
+            nc.scalar.dma_start(
+                out=table_sb[:],
+                in_=table.rearrange("(i e) j -> i (e j)", e=PARITY)
+                .unsqueeze(1)
+                .to_broadcast([ROWS, BATCH, PARITY * PAIRS]),
+            )
+
+        identity = keep.tile([P, P], F32)
+        make_identity(nc, identity[:])
+
+        cos_twice = keep.tile([P, PARITY * PAIRS, 2], BF16)
+        nc.scalar.copy(
+            out=cos_twice[:],
+            in_=cos_sb[:].unsqueeze(2).to_broadcast([P, PARITY * PAIRS, 2]),
+        )
+        minus_sin = keep.tile([P, PARITY * PAIRS], BF16)
+        nc.scalar.mul(out=minus_sin[:], in_=sin_sb[:], mul=-1.0)
+
+        x_as_words = x_sb[:].bitcast(F32)
+        x_codes = keep.tile([P, PARITY, P], U32, align_bytes=64)
+        x_scales = keep.tile([P, PARITY, P], U8, align_bytes=64)
+        words_per_row = MODEL // 2
+        for e in range(PARITY):
+            flipped = turned.tile([P, 2, P], F32)
+            for u in range(2):
+                nc.tensor.transpose(
+                    flipped[:, u, :],
+                    x_as_words[:, words_per_row * e + u : words_per_row * (e + 1) : 2],
+                    identity[:],
+                )
+            grouped = work.tile([P, P, PACK], BF16, align_bytes=64)
+            copy = nc.vector.tensor_copy if e % 2 == 0 else nc.scalar.copy
+            copy(out=grouped[:].bitcast(F32), in_=flipped[:].rearrange("p u m -> p m u"))
+            nc.vector.quantize_mx(
+                out=x_codes[:, e, :].bitcast(FP8X4),
+                scales=x_scales[:, e, :],
+                in_=grouped[:].rearrange("p m t -> p (m t)"),
+            )
+
+        cos_by_e = cos_twice[:].rearrange("p (e j) r -> p e (j r)", e=PARITY).unsqueeze(2)
+        sin_by_e = sin_sb[:].rearrange("p (e j) -> p e j", e=PARITY).unsqueeze(2)
+        minus_sin_by_e = minus_sin[:].rearrange("p (e j) -> p e j", e=PARITY).unsqueeze(2)
+        for first_head in range(0, HEADS, UNIT_HEADS):
+            for which, out in enumerate(outputs):
+                first_col = which * MODEL + first_head * HEAD_DIM
+                acc = sums.tile([P, PARITY, UNIT_HEADS, HEAD_DIM], F32)
+                for e in range(PARITY):
+                    nc.tensor.matmul_mx(
+                        out=acc[:, e].rearrange("p h d -> p (h d)"),
+                        lhsT=x_codes[:, e, :].bitcast(FP8X4),
+                        lhsT_scale=x_scales[:, e, :],
+                        rhs=w_words[:, 2 * first_col : 2 * (first_col + UNIT_COLS)].bitcast(
+                            FP4X4
+                        ),
+                        rhs_scale=w_scales[:, first_col : first_col + UNIT_COLS],
+                        start=True,
+                        stop=True,
+                    )
+
+                result = results.tile([P, UNIT_HEADS, PARITY, HEAD_DIM], F32)
+                if which == 2:
+                    nc.scalar.copy(out=result[:].rearrange("p h e d -> p e h d"), in_=acc[:])
+                    store_queue = nc.scalar
+                else:
+                    straight = work.tile([P, PARITY, UNIT_HEADS, HEAD_DIM], F32)
+                    nc.vector.tensor_tensor(
+                        out=straight[:],
+                        in0=acc[:],
+                        in1=cos_by_e.to_broadcast([P, PARITY, UNIT_HEADS, HEAD_DIM]),
+                        op=MULT,
+                    )
+                    crossed = work.tile([P, 2, PARITY, UNIT_HEADS, PAIRS], F32)
+                    members = acc[:].rearrange("p e h (j r) -> p e h j r", r=2)
+                    nc.vector.tensor_tensor(
+                        out=crossed[:, 0],
+                        in0=members[:, :, :, :, 1],
+                        in1=minus_sin_by_e.to_broadcast([P, PARITY, UNIT_HEADS, PAIRS]),
+                        op=MULT,
+                    )
+                    nc.vector.tensor_tensor(
+                        out=crossed[:, 1],
+                        in0=members[:, :, :, :, 0],
+                        in1=sin_by_e.to_broadcast([P, PARITY, UNIT_HEADS, PAIRS]),
+                        op=MULT,
+                    )
+                    nc.gpsimd.tensor_tensor(
+                        out=result[:].rearrange("p h e (j r) -> p e h j r", r=2),
+                        in0=straight[:].rearrange("p e h (j r) -> p e h j r", r=2),
+                        in1=crossed[:].rearrange("p r e h j -> p e h j r"),
+                        op=ADD,
+                    )
+                    store_queue = nc.sync
+
+                for b in range(BATCH):
+                    store_queue.dma_start(
+                        out=out[b, first_head : first_head + UNIT_HEADS].rearrange(
+                            "h (i e) d -> i h (e d)", e=PARITY
+                        ),
+                        in_=result[b:P:BATCH].rearrange("p h e d -> p h (e d)"),
+                    )

@@ -23,6 +23,9 @@ PARITY = 2
 ROWS = SEQ // PARITY
 UNIT_HEADS = 4
 UNIT_COLS = UNIT_HEADS * HEAD_DIM
+Q, K, V = 0, 1, 2
+UNITS = ((Q, 0), (V, 0), (V, UNIT_HEADS), (K, 0), (Q, UNIT_HEADS), (K, UNIT_HEADS))
+GPSIMD_SUMS = 3
 
 FLOPS = 2 * BATCH * SEQ * MODEL * 3 * MODEL
 
@@ -67,18 +70,18 @@ def tile_ropeflashattention_pa_s_kernel(
         identity = keep.tile([P, P], F32)
         make_identity(nc, identity[:])
 
-        cos_twice = keep.tile([P, PARITY * PAIRS, 2], BF16)
+        factors = keep.tile([P, 2, PARITY * PAIRS, 2], BF16)
         nc.scalar.copy(
-            out=cos_twice[:],
+            out=factors[:, 0],
             in_=cos_sb[:].unsqueeze(2).to_broadcast([P, PARITY * PAIRS, 2]),
         )
-        minus_sin = keep.tile([P, PARITY * PAIRS], BF16)
-        nc.scalar.mul(out=minus_sin[:], in_=sin_sb[:], mul=-1.0)
+        nc.scalar.copy(out=factors[:, 1, :, 0], in_=sin_sb[:])
+        nc.scalar.mul(out=factors[:, 1, :, 1], in_=sin_sb[:], mul=-1.0)
+        factors_by_e = factors[:].rearrange("p w (e j) r -> p w e (j r)", e=PARITY)
 
         x_as_words = x_sb[:].bitcast(F32)
-        x_codes = keep.tile([P, PARITY, P], U32, align_bytes=64)
-        x_scales = keep.tile([P, PARITY, P], U8, align_bytes=64)
         words_per_row = MODEL // 2
+        grouped = keep.tile([P, PARITY, P, PACK], BF16, align_bytes=64)
         for e in range(PARITY):
             flipped = turned.tile([P, 2, P], F32)
             for u in range(2):
@@ -87,73 +90,66 @@ def tile_ropeflashattention_pa_s_kernel(
                     x_as_words[:, words_per_row * e + u : words_per_row * (e + 1) : 2],
                     identity[:],
                 )
-            grouped = work.tile([P, P, PACK], BF16, align_bytes=64)
-            copy = nc.vector.tensor_copy if e % 2 == 0 else nc.scalar.copy
-            copy(out=grouped[:].bitcast(F32), in_=flipped[:].rearrange("p u m -> p m u"))
+            nc.vector.tensor_copy(
+                out=grouped[:, e].bitcast(F32), in_=flipped[:].rearrange("p u m -> p m u")
+            )
+        x_codes = keep.tile([P, PARITY, P], U32, align_bytes=64)
+        x_scales = keep.tile([P, PARITY, P], U8, align_bytes=64)
+        for e in range(PARITY):
             nc.vector.quantize_mx(
                 out=x_codes[:, e, :].bitcast(FP8X4),
                 scales=x_scales[:, e, :],
-                in_=grouped[:].rearrange("p m t -> p (m t)"),
+                in_=grouped[:, e].rearrange("p m t -> p (m t)"),
             )
 
-        cos_by_e = cos_twice[:].rearrange("p (e j) r -> p e (j r)", e=PARITY).unsqueeze(2)
-        sin_by_e = sin_sb[:].rearrange("p (e j) -> p e j", e=PARITY).unsqueeze(2)
-        minus_sin_by_e = minus_sin[:].rearrange("p (e j) -> p e j", e=PARITY).unsqueeze(2)
-        for first_head in range(0, HEADS, UNIT_HEADS):
-            for which, out in enumerate(outputs):
-                first_col = which * MODEL + first_head * HEAD_DIM
-                acc = sums.tile([P, PARITY, UNIT_HEADS, HEAD_DIM], F32)
-                for e in range(PARITY):
-                    nc.tensor.matmul_mx(
-                        out=acc[:, e].rearrange("p h d -> p (h d)"),
-                        lhsT=x_codes[:, e, :].bitcast(FP8X4),
-                        lhsT_scale=x_scales[:, e, :],
-                        rhs=w_words[:, 2 * first_col : 2 * (first_col + UNIT_COLS)].bitcast(
-                            FP4X4
-                        ),
-                        rhs_scale=w_scales[:, first_col : first_col + UNIT_COLS],
-                        start=True,
-                        stop=True,
-                    )
-
-                result = results.tile([P, UNIT_HEADS, PARITY, HEAD_DIM], F32)
-                if which == 2:
-                    nc.scalar.copy(out=result[:].rearrange("p h e d -> p e h d"), in_=acc[:])
-                    store_queue = nc.scalar
+        rotated_units = 0
+        for which, first_head in UNITS:
+            first_col = which * MODEL + first_head * HEAD_DIM
+            result = results.tile([P, UNIT_HEADS, PARITY, HEAD_DIM], F32)
+            if which != V:
+                products = work.tile([P, 2, PARITY, UNIT_HEADS, HEAD_DIM], F32)
+            for e in range(PARITY):
+                acc = sums.tile([P, UNIT_HEADS, HEAD_DIM], F32)
+                nc.tensor.matmul_mx(
+                    out=acc[:].rearrange("p h d -> p (h d)"),
+                    lhsT=x_codes[:, e, :].bitcast(FP8X4),
+                    lhsT_scale=x_scales[:, e, :],
+                    rhs=w_words[:, 2 * first_col : 2 * (first_col + UNIT_COLS)].bitcast(FP4X4),
+                    rhs_scale=w_scales[:, first_col : first_col + UNIT_COLS],
+                    start=True,
+                    stop=True,
+                )
+                if which == V:
+                    nc.scalar.copy(out=result[:, :, e, :], in_=acc[:])
                 else:
-                    straight = work.tile([P, PARITY, UNIT_HEADS, HEAD_DIM], F32)
                     nc.vector.tensor_tensor(
-                        out=straight[:],
-                        in0=acc[:],
-                        in1=cos_by_e.to_broadcast([P, PARITY, UNIT_HEADS, HEAD_DIM]),
+                        out=products[:, :, e],
+                        in0=acc[:].unsqueeze(1).to_broadcast([P, 2, UNIT_HEADS, HEAD_DIM]),
+                        in1=factors_by_e[:, :, e]
+                        .unsqueeze(2)
+                        .to_broadcast([P, 2, UNIT_HEADS, HEAD_DIM]),
                         op=MULT,
                     )
-                    crossed = work.tile([P, 2, PARITY, UNIT_HEADS, PAIRS], F32)
-                    members = acc[:].rearrange("p e h (j r) -> p e h j r", r=2)
-                    nc.vector.tensor_tensor(
-                        out=crossed[:, 0],
-                        in0=members[:, :, :, :, 1],
-                        in1=minus_sin_by_e.to_broadcast([P, PARITY, UNIT_HEADS, PAIRS]),
-                        op=MULT,
-                    )
-                    nc.vector.tensor_tensor(
-                        out=crossed[:, 1],
-                        in0=members[:, :, :, :, 0],
-                        in1=sin_by_e.to_broadcast([P, PARITY, UNIT_HEADS, PAIRS]),
-                        op=MULT,
-                    )
-                    nc.gpsimd.tensor_tensor(
-                        out=result[:].rearrange("p h e (j r) -> p e h j r", r=2),
-                        in0=straight[:].rearrange("p e h (j r) -> p e h j r", r=2),
-                        in1=crossed[:].rearrange("p r e h j -> p e h j r"),
-                        op=ADD,
-                    )
-                    store_queue = nc.sync
 
-                for b in range(BATCH):
-                    store_queue.dma_start(
-                        out=out[b, first_head : first_head + UNIT_HEADS].rearrange(
-                            "h (i e) d -> i h (e d)", e=PARITY
-                        ),
-                        in_=result[b:P:BATCH].rearrange("p h e d -> p h (e d)"),
-                    )
+            if which == V:
+                store_queue = nc.scalar
+            else:
+                summer = nc.gpsimd if rotated_units < GPSIMD_SUMS else nc.vector
+                rotated_units += 1
+                own = products[:, 0].rearrange("p e h (j r) -> p e h j r", r=2)
+                other = products[:, 1].rearrange("p e h (j r) -> p e h j r", r=2)
+                summer.tensor_tensor(
+                    out=result[:].rearrange("p h e (j r) -> p e h j r", r=2),
+                    in0=own,
+                    in1=other[:, :, :, :, ::-1],
+                    op=ADD,
+                )
+                store_queue = nc.sync
+
+            for b in range(BATCH):
+                store_queue.dma_start(
+                    out=outputs[which][b, first_head : first_head + UNIT_HEADS].rearrange(
+                        "h (i e) d -> i h (e d)", e=PARITY
+                    ),
+                    in_=result[b:P:BATCH].rearrange("p h e d -> p h (e d)"),
+                )

@@ -26,6 +26,7 @@ UNIT_COLS = UNIT_HEADS * HEAD_DIM
 Q, K, V = 0, 1, 2
 UNITS = ((Q, 0), (V, 0), (V, UNIT_HEADS), (K, 0), (Q, UNIT_HEADS), (K, UNIT_HEADS))
 GPSIMD_SUMS = 3
+WARM_UP = 6
 
 FLOPS = 2 * BATCH * SEQ * MODEL * 3 * MODEL
 
@@ -69,6 +70,16 @@ def tile_ropeflashattention_pa_s_kernel(
 
         identity = keep.tile([P, P], F32)
         make_identity(nc, identity[:])
+
+        idle_product = turned.tile([P, 2, P], F32, tag="flipped")
+        for repeat in range(WARM_UP):
+            nc.tensor.matmul(
+                out=idle_product[:, 0, :],
+                lhsT=identity[:],
+                rhs=identity[:],
+                start=True,
+                stop=True,
+            )
 
         factors = keep.tile([P, 2, PARITY * PAIRS, 2], BF16)
         nc.scalar.copy(

@@ -24,9 +24,9 @@ ROWS = SEQ // PARITY
 UNIT_HEADS = 4
 UNIT_COLS = UNIT_HEADS * HEAD_DIM
 Q, K, V = 0, 1, 2
-UNITS = ((Q, 0), (V, 0), (V, UNIT_HEADS), (K, 0), (Q, UNIT_HEADS), (K, UNIT_HEADS))
+ROTATED = ((Q, 0), (K, 0), (Q, UNIT_HEADS), (K, UNIT_HEADS))
+COPIED = ((V, 0), (V, UNIT_HEADS))
 GPSIMD_SUMS = 3
-WARM_UP = 6
 
 FLOPS = 2 * BATCH * SEQ * MODEL * 3 * MODEL
 
@@ -71,23 +71,13 @@ def tile_ropeflashattention_pa_s_kernel(
         identity = keep.tile([P, P], F32)
         make_identity(nc, identity[:])
 
-        idle_product = turned.tile([P, 2, P], F32, tag="flipped")
-        for repeat in range(WARM_UP):
-            nc.tensor.matmul(
-                out=idle_product[:, 0, :],
-                lhsT=identity[:],
-                rhs=identity[:],
-                start=True,
-                stop=True,
-            )
-
         factors = keep.tile([P, 2, PARITY * PAIRS, 2], BF16)
-        nc.scalar.copy(
+        nc.vector.tensor_copy(
             out=factors[:, 0],
             in_=cos_sb[:].unsqueeze(2).to_broadcast([P, PARITY * PAIRS, 2]),
         )
-        nc.scalar.copy(out=factors[:, 1, :, 0], in_=sin_sb[:])
-        nc.scalar.mul(out=factors[:, 1, :, 1], in_=sin_sb[:], mul=-1.0)
+        nc.vector.tensor_copy(out=factors[:, 1, :, 0], in_=sin_sb[:])
+        nc.vector.tensor_scalar_mul(out=factors[:, 1, :, 1], in0=sin_sb[:], scalar1=-1.0)
         factors_by_e = factors[:].rearrange("p w (e j) r -> p w e (j r)", e=PARITY)
 
         x_as_words = x_sb[:].bitcast(F32)
@@ -101,7 +91,7 @@ def tile_ropeflashattention_pa_s_kernel(
                     x_as_words[:, words_per_row * e + u : words_per_row * (e + 1) : 2],
                     identity[:],
                 )
-            nc.vector.tensor_copy(
+            nc.scalar.copy(
                 out=grouped[:, e].bitcast(F32), in_=flipped[:].rearrange("p u m -> p m u")
             )
         x_codes = keep.tile([P, PARITY, P], U32, align_bytes=64)
@@ -113,54 +103,59 @@ def tile_ropeflashattention_pa_s_kernel(
                 in_=grouped[:, e].rearrange("p m t -> p (m t)"),
             )
 
-        rotated_units = 0
-        for which, first_head in UNITS:
+        def project(which, first_head, e):
             first_col = which * MODEL + first_head * HEAD_DIM
-            result = results.tile([P, UNIT_HEADS, PARITY, HEAD_DIM], F32)
-            if which != V:
-                products = work.tile([P, 2, PARITY, UNIT_HEADS, HEAD_DIM], F32)
-            for e in range(PARITY):
-                acc = sums.tile([P, UNIT_HEADS, HEAD_DIM], F32)
-                nc.tensor.matmul_mx(
-                    out=acc[:].rearrange("p h d -> p (h d)"),
-                    lhsT=x_codes[:, e, :].bitcast(FP8X4),
-                    lhsT_scale=x_scales[:, e, :],
-                    rhs=w_words[:, 2 * first_col : 2 * (first_col + UNIT_COLS)].bitcast(FP4X4),
-                    rhs_scale=w_scales[:, first_col : first_col + UNIT_COLS],
-                    start=True,
-                    stop=True,
-                )
-                if which == V:
-                    nc.scalar.copy(out=result[:, :, e, :], in_=acc[:])
-                else:
-                    nc.vector.tensor_tensor(
-                        out=products[:, :, e],
-                        in0=acc[:].unsqueeze(1).to_broadcast([P, 2, UNIT_HEADS, HEAD_DIM]),
-                        in1=factors_by_e[:, :, e]
-                        .unsqueeze(2)
-                        .to_broadcast([P, 2, UNIT_HEADS, HEAD_DIM]),
-                        op=MULT,
-                    )
+            acc = sums.tile([P, UNIT_HEADS, HEAD_DIM], F32)
+            nc.tensor.matmul_mx(
+                out=acc[:].rearrange("p h d -> p (h d)"),
+                lhsT=x_codes[:, e, :].bitcast(FP8X4),
+                lhsT_scale=x_scales[:, e, :],
+                rhs=w_words[:, 2 * first_col : 2 * (first_col + UNIT_COLS)].bitcast(FP4X4),
+                rhs_scale=w_scales[:, first_col : first_col + UNIT_COLS],
+                start=True,
+                stop=True,
+            )
+            return acc
 
-            if which == V:
-                store_queue = nc.scalar
-            else:
-                summer = nc.gpsimd if rotated_units < GPSIMD_SUMS else nc.vector
-                rotated_units += 1
-                own = products[:, 0].rearrange("p e h (j r) -> p e h j r", r=2)
-                other = products[:, 1].rearrange("p e h (j r) -> p e h j r", r=2)
-                summer.tensor_tensor(
-                    out=result[:].rearrange("p h e (j r) -> p e h j r", r=2),
-                    in0=own,
-                    in1=other[:, :, :, :, ::-1],
-                    op=ADD,
-                )
-                store_queue = nc.sync
-
+        def store(queue, which, first_head, result):
             for b in range(BATCH):
-                store_queue.dma_start(
+                queue.dma_start(
                     out=outputs[which][b, first_head : first_head + UNIT_HEADS].rearrange(
                         "h (i e) d -> i h (e d)", e=PARITY
                     ),
                     in_=result[b:P:BATCH].rearrange("p h e d -> p h (e d)"),
                 )
+
+        for step, (which, first_head) in enumerate(ROTATED):
+            rotated = results.tile([P, UNIT_HEADS, PARITY, HEAD_DIM], F32, tag="result")
+            products = work.tile([P, 2, PARITY, UNIT_HEADS, HEAD_DIM], F32)
+            riders = COPIED[step : step + 1]
+            if riders:
+                copied = results.tile([P, UNIT_HEADS, PARITY, HEAD_DIM], F32, tag="result")
+            for e in range(PARITY):
+                acc = project(which, first_head, e)
+                nc.vector.tensor_tensor(
+                    out=products[:, :, e],
+                    in0=acc[:].unsqueeze(1).to_broadcast([P, 2, UNIT_HEADS, HEAD_DIM]),
+                    in1=factors_by_e[:, :, e]
+                    .unsqueeze(2)
+                    .to_broadcast([P, 2, UNIT_HEADS, HEAD_DIM]),
+                    op=MULT,
+                )
+                for rider_which, rider_head in riders:
+                    rider_acc = project(rider_which, rider_head, e)
+                    nc.scalar.copy(out=copied[:, :, e, :], in_=rider_acc[:])
+
+            for rider_which, rider_head in riders:
+                store(nc.scalar, rider_which, rider_head, copied)
+
+            summer = nc.gpsimd if step < GPSIMD_SUMS else nc.vector
+            own = products[:, 0].rearrange("p e h (j r) -> p e h j r", r=2)
+            other = products[:, 1].rearrange("p e h (j r) -> p e h j r", r=2)
+            summer.tensor_tensor(
+                out=rotated[:].rearrange("p h e (j r) -> p e h j r", r=2),
+                in0=own,
+                in1=other[:, :, :, :, ::-1],
+                op=ADD,
+            )
+            store(nc.sync, which, first_head, rotated)

@@ -24,9 +24,6 @@ ROWS = SEQ // PARITY
 UNIT_HEADS = 4
 UNIT_COLS = UNIT_HEADS * HEAD_DIM
 Q, K, V = 0, 1, 2
-ROTATED = ((Q, 0), (K, 0), (Q, UNIT_HEADS), (K, UNIT_HEADS))
-COPIED = ((V, 0), (V, UNIT_HEADS))
-GPSIMD_SUMS = 3
 
 FLOPS = 2 * BATCH * SEQ * MODEL * 3 * MODEL
 
@@ -40,13 +37,25 @@ def tile_ropeflashattention_pa_s_kernel(
     with tc.tile_pool(name="keep", bufs=1) as keep, tc.tile_pool(
         name="work", bufs=4
     ) as work, tc.tile_pool(name="results", bufs=6) as results, tc.psum_pool(
-        name="turned", bufs=2
-    ) as turned, tc.psum_pool(name="sums", bufs=6) as sums:
+        name="banks", bufs=8
+    ) as banks, tc.manual_schedule():
         x_sb = keep.tile([P, PARITY * MODEL], BF16)
         nc.sync.dma_start(
             out=x_sb[:], in_=x.rearrange("b (i e) k -> i b (e k)", e=PARITY)
         )
-
+        cos_sb = keep.tile([P, PARITY * PAIRS], BF16)
+        sin_sb = keep.tile([P, PARITY * PAIRS], BF16)
+        for table_sb, table in ((cos_sb, cos), (sin_sb, sin)):
+            nc.sync.dma_start(
+                out=table_sb[:],
+                in_=table.rearrange("(i e) j -> i (e j)", e=PARITY)
+                .unsqueeze(1)
+                .to_broadcast([ROWS, BATCH, PARITY * PAIRS]),
+            )
+        w_q = keep.tile([P, 2 * MODEL], U8, align_bytes=64)
+        nc.sync.dma_start(
+            out=w_q[:].bitcast(I32), in_=w_qkv_words[0][:, 0 : 2 * MODEL].bitcast(I32)
+        )
         w_scales = keep.tile([P, 3 * MODEL], U8, align_bytes=64)
         nc.vector.memset(w_scales[:].bitcast(I32), 0)
         for quadrant in range(4):
@@ -54,19 +63,11 @@ def tile_ropeflashattention_pa_s_kernel(
                 out=w_scales[32 * quadrant : 32 * quadrant + 4, :].bitcast(I32),
                 in_=w_qkv_scales[0, 4 * quadrant : 4 * quadrant + 4, :].bitcast(I32),
             )
-
-        w_words = keep.tile([P, 2 * 3 * MODEL], U8, align_bytes=64)
-        nc.sync.dma_start(out=w_words[:].bitcast(I32), in_=w_qkv_words[0].bitcast(I32))
-
-        cos_sb = keep.tile([P, PARITY * PAIRS], BF16)
-        sin_sb = keep.tile([P, PARITY * PAIRS], BF16)
-        for table_sb, table in ((cos_sb, cos), (sin_sb, sin)):
-            nc.scalar.dma_start(
-                out=table_sb[:],
-                in_=table.rearrange("(i e) j -> i (e j)", e=PARITY)
-                .unsqueeze(1)
-                .to_broadcast([ROWS, BATCH, PARITY * PAIRS]),
-            )
+        w_kv = keep.tile([P, 4 * MODEL], U8, align_bytes=64)
+        nc.sync.dma_start(
+            out=w_kv[:].bitcast(I32),
+            in_=w_qkv_words[0][:, 2 * MODEL : 6 * MODEL].bitcast(I32),
+        )
 
         identity = keep.tile([P, P], F32)
         make_identity(nc, identity[:])
@@ -84,7 +85,7 @@ def tile_ropeflashattention_pa_s_kernel(
         words_per_row = MODEL // 2
         grouped = keep.tile([P, PARITY, P, PACK], BF16, align_bytes=64)
         for e in range(PARITY):
-            flipped = turned.tile([P, 2, P], F32)
+            flipped = banks.tile([P, 2, P], F32, tag="bank")
             for u in range(2):
                 nc.tensor.transpose(
                     flipped[:, u, :],
@@ -103,21 +104,27 @@ def tile_ropeflashattention_pa_s_kernel(
                 in_=grouped[:, e].rearrange("p m t -> p (m t)"),
             )
 
-        def project(which, first_head, e):
+        def project(unit, e):
+            which, first_head = unit
             first_col = which * MODEL + first_head * HEAD_DIM
-            acc = sums.tile([P, UNIT_HEADS, HEAD_DIM], F32)
+            if which == Q:
+                codes, code_col = w_q, first_col
+            else:
+                codes, code_col = w_kv, first_col - MODEL
+            acc = banks.tile([P, UNIT_HEADS, HEAD_DIM], F32, tag="bank")
             nc.tensor.matmul_mx(
                 out=acc[:].rearrange("p h d -> p (h d)"),
                 lhsT=x_codes[:, e, :].bitcast(FP8X4),
                 lhsT_scale=x_scales[:, e, :],
-                rhs=w_words[:, 2 * first_col : 2 * (first_col + UNIT_COLS)].bitcast(FP4X4),
+                rhs=codes[:, 2 * code_col : 2 * (code_col + UNIT_COLS)].bitcast(FP4X4),
                 rhs_scale=w_scales[:, first_col : first_col + UNIT_COLS],
                 start=True,
                 stop=True,
             )
             return acc
 
-        def store(queue, which, first_head, result):
+        def store(queue, unit, result):
+            which, first_head = unit
             for b in range(BATCH):
                 queue.dma_start(
                     out=outputs[which][b, first_head : first_head + UNIT_HEADS].rearrange(
@@ -126,36 +133,57 @@ def tile_ropeflashattention_pa_s_kernel(
                     in_=result[b:P:BATCH].rearrange("p h e d -> p h (e d)"),
                 )
 
-        for step, (which, first_head) in enumerate(ROTATED):
-            rotated = results.tile([P, UNIT_HEADS, PARITY, HEAD_DIM], F32, tag="result")
-            products = work.tile([P, 2, PARITY, UNIT_HEADS, HEAD_DIM], F32)
-            riders = COPIED[step : step + 1]
-            if riders:
-                copied = results.tile([P, UNIT_HEADS, PARITY, HEAD_DIM], F32, tag="result")
+        def multiply(accs):
+            products = work.tile([P, 2, PARITY, UNIT_HEADS, HEAD_DIM], F32, tag="products")
             for e in range(PARITY):
-                acc = project(which, first_head, e)
                 nc.vector.tensor_tensor(
                     out=products[:, :, e],
-                    in0=acc[:].unsqueeze(1).to_broadcast([P, 2, UNIT_HEADS, HEAD_DIM]),
+                    in0=accs[e][:].unsqueeze(1).to_broadcast([P, 2, UNIT_HEADS, HEAD_DIM]),
                     in1=factors_by_e[:, :, e]
                     .unsqueeze(2)
                     .to_broadcast([P, 2, UNIT_HEADS, HEAD_DIM]),
                     op=MULT,
                 )
-                for rider_which, rider_head in riders:
-                    rider_acc = project(rider_which, rider_head, e)
-                    nc.scalar.copy(out=copied[:, :, e, :], in_=rider_acc[:])
+            return products
 
-            for rider_which, rider_head in riders:
-                store(nc.scalar, rider_which, rider_head, copied)
-
-            summer = nc.gpsimd if step < GPSIMD_SUMS else nc.vector
+        def add(engine, products):
+            rotated = results.tile([P, UNIT_HEADS, PARITY, HEAD_DIM], F32, tag="result")
             own = products[:, 0].rearrange("p e h (j r) -> p e h j r", r=2)
             other = products[:, 1].rearrange("p e h (j r) -> p e h j r", r=2)
-            summer.tensor_tensor(
+            engine.tensor_tensor(
                 out=rotated[:].rearrange("p h e (j r) -> p e h j r", r=2),
                 in0=own,
                 in1=other[:, :, :, :, ::-1],
                 op=ADD,
             )
-            store(nc.sync, which, first_head, rotated)
+            return rotated
+
+        def copy_out(accs):
+            copied = results.tile([P, UNIT_HEADS, PARITY, HEAD_DIM], F32, tag="result")
+            for e in range(PARITY):
+                nc.scalar.copy(out=copied[:, :, e, :], in_=accs[e][:])
+            return copied
+
+        both = range(PARITY)
+        q0, q4, k0, k4, v0, v4 = (Q, 0), (Q, 4), (K, 0), (K, 4), (V, 0), (V, 4)
+
+        acc_q0 = [project(q0, e) for e in both]
+        acc_q4 = [project(q4, e) for e in both]
+        acc_v0 = [project(v0, e) for e in both]
+        prod_q0 = multiply(acc_q0)
+        acc_k0 = [project(k0, e) for e in both]
+        store(nc.scalar, v0, copy_out(acc_v0))
+        rot_q0 = add(nc.gpsimd, prod_q0)
+        store(nc.sync, q0, rot_q0)
+        acc_v4 = [project(v4, e) for e in both]
+        prod_q4 = multiply(acc_q4)
+        store(nc.scalar, v4, copy_out(acc_v4))
+        rot_q4 = add(nc.gpsimd, prod_q4)
+        store(nc.sync, q4, rot_q4)
+        acc_k4 = [project(k4, e) for e in both]
+        prod_k0 = multiply(acc_k0)
+        rot_k0 = add(nc.gpsimd, prod_k0)
+        prod_k4 = multiply(acc_k4)
+        rot_k4 = add(nc.vector, prod_k4)
+        store(nc.scalar, k4, rot_k4)
+        store(nc.sync, k0, rot_k0)

@@ -36,7 +36,7 @@ def tile_ropeflashattention_pa_s_kernel(
 
     with tc.tile_pool(name="keep", bufs=1) as keep, tc.tile_pool(
         name="work", bufs=4
-    ) as work, tc.tile_pool(name="results", bufs=6) as results, tc.psum_pool(
+    ) as work, tc.tile_pool(name="results", bufs=9) as results, tc.psum_pool(
         name="banks", bufs=8
     ) as banks, tc.manual_schedule():
         x_sb = keep.tile([P, PARITY * MODEL], BF16)
@@ -52,9 +52,11 @@ def tile_ropeflashattention_pa_s_kernel(
                 .unsqueeze(1)
                 .to_broadcast([ROWS, BATCH, PARITY * PAIRS]),
             )
-        w_q = keep.tile([P, 2 * MODEL], U8, align_bytes=64)
+        w_words = keep.tile([P, 3, 2 * MODEL], U8, align_bytes=64)
+        w_in_hbm = w_qkv_words[0].rearrange("p (w c) -> p w c", w=3)
         nc.sync.dma_start(
-            out=w_q[:].bitcast(I32), in_=w_qkv_words[0][:, 0 : 2 * MODEL].bitcast(I32)
+            out=w_words[:, Q : V + 1 : 2, :].bitcast(I32),
+            in_=w_in_hbm[:, Q : V + 1 : 2, :].bitcast(I32),
         )
         w_scales = keep.tile([P, 3 * MODEL], U8, align_bytes=64)
         nc.vector.memset(w_scales[:].bitcast(I32), 0)
@@ -63,10 +65,8 @@ def tile_ropeflashattention_pa_s_kernel(
                 out=w_scales[32 * quadrant : 32 * quadrant + 4, :].bitcast(I32),
                 in_=w_qkv_scales[0, 4 * quadrant : 4 * quadrant + 4, :].bitcast(I32),
             )
-        w_kv = keep.tile([P, 4 * MODEL], U8, align_bytes=64)
         nc.sync.dma_start(
-            out=w_kv[:].bitcast(I32),
-            in_=w_qkv_words[0][:, 2 * MODEL : 6 * MODEL].bitcast(I32),
+            out=w_words[:, K, :].bitcast(I32), in_=w_in_hbm[:, K, :].bitcast(I32)
         )
 
         identity = keep.tile([P, P], F32)
@@ -83,8 +83,10 @@ def tile_ropeflashattention_pa_s_kernel(
 
         x_as_words = x_sb[:].bitcast(F32)
         words_per_row = MODEL // 2
-        grouped = keep.tile([P, PARITY, P, PACK], BF16, align_bytes=64)
+        grouped = []
         for e in range(PARITY):
+            grouped_e = keep.tile([P, P, PACK], BF16, align_bytes=64, name="grouped%d" % e)
+            grouped.append(grouped_e)
             flipped = banks.tile([P, 2, P], F32, tag="bank")
             for u in range(2):
                 nc.tensor.transpose(
@@ -93,51 +95,52 @@ def tile_ropeflashattention_pa_s_kernel(
                     identity[:],
                 )
             nc.scalar.copy(
-                out=grouped[:, e].bitcast(F32), in_=flipped[:].rearrange("p u m -> p m u")
+                out=grouped_e[:].bitcast(F32), in_=flipped[:].rearrange("p u m -> p m u")
             )
-        x_codes = keep.tile([P, PARITY, P], U32, align_bytes=64)
-        x_scales = keep.tile([P, PARITY, P], U8, align_bytes=64)
+        x_codes = []
+        x_scales = []
         for e in range(PARITY):
+            codes_e = keep.tile([P, P], U32, align_bytes=64, name="x_codes%d" % e)
+            scales_e = keep.tile([P, P], U8, align_bytes=64, name="x_scales%d" % e)
             nc.vector.quantize_mx(
-                out=x_codes[:, e, :].bitcast(FP8X4),
-                scales=x_scales[:, e, :],
-                in_=grouped[:, e].rearrange("p m t -> p (m t)"),
+                out=codes_e[:].bitcast(FP8X4),
+                scales=scales_e[:],
+                in_=grouped[e][:].rearrange("p m t -> p (m t)"),
             )
+            x_codes.append(codes_e)
+            x_scales.append(scales_e)
 
         def project(unit, e):
             which, first_head = unit
-            first_col = which * MODEL + first_head * HEAD_DIM
-            if which == Q:
-                codes, code_col = w_q, first_col
-            else:
-                codes, code_col = w_kv, first_col - MODEL
+            head_col = first_head * HEAD_DIM
+            first_col = which * MODEL + head_col
             acc = banks.tile([P, UNIT_HEADS, HEAD_DIM], F32, tag="bank")
             nc.tensor.matmul_mx(
                 out=acc[:].rearrange("p h d -> p (h d)"),
-                lhsT=x_codes[:, e, :].bitcast(FP8X4),
-                lhsT_scale=x_scales[:, e, :],
-                rhs=codes[:, 2 * code_col : 2 * (code_col + UNIT_COLS)].bitcast(FP4X4),
+                lhsT=x_codes[e][:].bitcast(FP8X4),
+                lhsT_scale=x_scales[e][:],
+                rhs=w_words[:, which, 2 * head_col : 2 * (head_col + UNIT_COLS)].bitcast(FP4X4),
                 rhs_scale=w_scales[:, first_col : first_col + UNIT_COLS],
                 start=True,
                 stop=True,
             )
             return acc
 
-        def store(queue, unit, result):
-            which, first_head = unit
+        def store(queues, which, first_head, result):
+            heads = result[:].shape[1]
             for b in range(BATCH):
-                queue.dma_start(
-                    out=outputs[which][b, first_head : first_head + UNIT_HEADS].rearrange(
+                queues[b].dma_start(
+                    out=outputs[which][b, first_head : first_head + heads].rearrange(
                         "h (i e) d -> i h (e d)", e=PARITY
                     ),
                     in_=result[b:P:BATCH].rearrange("p h e d -> p h (e d)"),
                 )
 
         def multiply(accs):
-            products = work.tile([P, 2, PARITY, UNIT_HEADS, HEAD_DIM], F32, tag="products")
+            products = work.tile([P, 2, UNIT_HEADS, PARITY, HEAD_DIM], F32, tag="products")
             for e in range(PARITY):
                 nc.vector.tensor_tensor(
-                    out=products[:, :, e],
+                    out=products[:, :, :, e, :],
                     in0=accs[e][:].unsqueeze(1).to_broadcast([P, 2, UNIT_HEADS, HEAD_DIM]),
                     in1=factors_by_e[:, :, e]
                     .unsqueeze(2)
@@ -146,16 +149,19 @@ def tile_ropeflashattention_pa_s_kernel(
                 )
             return products
 
-        def add(engine, products):
-            rotated = results.tile([P, UNIT_HEADS, PARITY, HEAD_DIM], F32, tag="result")
-            own = products[:, 0].rearrange("p e h (j r) -> p e h j r", r=2)
-            other = products[:, 1].rearrange("p e h (j r) -> p e h j r", r=2)
+        def add(engine, products, heads, rotated, at=0):
+            h0, h1 = heads
+            own = products[:, 0, h0:h1].rearrange("p h e (j r) -> p (h e j) r", r=2)
+            other = products[:, 1, h0:h1].rearrange("p h e (j r) -> p (h e j) r", r=2)
             engine.tensor_tensor(
-                out=rotated[:].rearrange("p h e (j r) -> p e h j r", r=2),
+                out=rotated[:, at : at + h1 - h0].rearrange("p h e (j r) -> p (h e j) r", r=2),
                 in0=own,
-                in1=other[:, :, :, :, ::-1],
+                in1=other[:, :, ::-1],
                 op=ADD,
             )
+
+        def new_result(heads):
+            rotated = results.tile([P, heads, PARITY, HEAD_DIM], F32, tag="result")
             return rotated
 
         def copy_out(accs):
@@ -167,23 +173,35 @@ def tile_ropeflashattention_pa_s_kernel(
         both = range(PARITY)
         q0, q4, k0, k4, v0, v4 = (Q, 0), (Q, 4), (K, 0), (K, 4), (V, 0), (V, 4)
 
+        sync2 = (nc.sync, nc.sync)
+        first_half, second_half = (0, 2), (2, 4)
+
+        whole = (0, UNIT_HEADS)
         acc_q0 = [project(q0, e) for e in both]
-        acc_q4 = [project(q4, e) for e in both]
         acc_v0 = [project(v0, e) for e in both]
-        prod_q0 = multiply(acc_q0)
-        acc_k0 = [project(k0, e) for e in both]
-        store(nc.scalar, v0, copy_out(acc_v0))
-        rot_q0 = add(nc.gpsimd, prod_q0)
-        store(nc.sync, q0, rot_q0)
+        acc_q4 = [project(q4, e) for e in both]
         acc_v4 = [project(v4, e) for e in both]
+        prod_q0 = multiply(acc_q0)
+        store(sync2, V, 0, copy_out(acc_v0))
+        acc_k0 = [project(k0, e) for e in both]
+        store(sync2, V, 4, copy_out(acc_v4))
+        rot_q0 = new_result(4)
+        add(nc.gpsimd, prod_q0, whole, rot_q0)
+        store(sync2, Q, 0, rot_q0)
         prod_q4 = multiply(acc_q4)
-        store(nc.scalar, v4, copy_out(acc_v4))
-        rot_q4 = add(nc.gpsimd, prod_q4)
-        store(nc.sync, q4, rot_q4)
         acc_k4 = [project(k4, e) for e in both]
+        rot_q4 = new_result(4)
+        add(nc.gpsimd, prod_q4, whole, rot_q4)
+        store(sync2, Q, 4, rot_q4)
         prod_k0 = multiply(acc_k0)
-        rot_k0 = add(nc.gpsimd, prod_k0)
+        rot_k01 = new_result(2)
+        add(nc.gpsimd, prod_k0, first_half, rot_k01)
+        store(sync2, K, 0, rot_k01)
         prod_k4 = multiply(acc_k4)
-        rot_k4 = add(nc.vector, prod_k4)
-        store(nc.scalar, k4, rot_k4)
-        store(nc.sync, k0, rot_k0)
+        rot_k25 = new_result(4)
+        add(nc.vector, prod_k0, second_half, rot_k25, 0)
+        add(nc.vector, prod_k4, first_half, rot_k25, 2)
+        store((nc.scalar, nc.sync), K, 2, rot_k25)
+        rot_k67 = new_result(2)
+        add(nc.vector, prod_k4, second_half, rot_k67)
+        store((nc.scalar, nc.sync), K, 6, rot_k67)

@@ -24,6 +24,7 @@ ROWS = SEQ // PARITY
 UNIT_HEADS = 4
 UNIT_COLS = UNIT_HEADS * HEAD_DIM
 Q, K, V = 0, 1, 2
+WARM_UP = 4
 
 FLOPS = 2 * BATCH * SEQ * MODEL * 3 * MODEL
 
@@ -68,6 +69,12 @@ def tile_ropeflashattention_pa_s_kernel(
         nc.sync.dma_start(
             out=w_words[:, K, :].bitcast(I32), in_=w_in_hbm[:, K, :].bitcast(I32)
         )
+
+        zeros = keep.tile([P, P], F32)
+        nc.gpsimd.memset(zeros[:], 0.0)
+        for warm in range(WARM_UP):
+            unused = banks.tile([P, P], F32, tag="bank")
+            nc.tensor.matmul(unused[:], lhsT=zeros[:], rhs=zeros[:], start=True, stop=True)
 
         identity = keep.tile([P, P], F32)
         make_identity(nc, identity[:])

@@ -79,14 +79,14 @@ def tile_ropeflashattention_pa_s_kernel(
         identity = keep.tile([P, P], F32)
         make_identity(nc, identity[:])
 
-        factors = keep.tile([P, 2, PARITY * PAIRS, 2], BF16)
+        factors = keep.tile([P, PARITY * PAIRS, 4], BF16)
         nc.vector.tensor_copy(
-            out=factors[:, 0],
+            out=factors[:, :, 0:4:3],
             in_=cos_sb[:].unsqueeze(2).to_broadcast([P, PARITY * PAIRS, 2]),
         )
-        nc.vector.tensor_copy(out=factors[:, 1, :, 0], in_=sin_sb[:])
-        nc.vector.tensor_scalar_mul(out=factors[:, 1, :, 1], in0=sin_sb[:], scalar1=-1.0)
-        factors_by_e = factors[:].rearrange("p w (e j) r -> p w e (j r)", e=PARITY)
+        nc.vector.tensor_scalar_mul(out=factors[:, :, 1], in0=sin_sb[:], scalar1=-1.0)
+        nc.vector.tensor_copy(out=factors[:, :, 2], in_=sin_sb[:])
+        factors_by_e = factors[:].rearrange("p (e j) (a u) -> p e j a u", e=PARITY, u=2)
 
         x_as_words = x_sb[:].bitcast(F32)
         words_per_row = MODEL // 2
@@ -144,26 +144,27 @@ def tile_ropeflashattention_pa_s_kernel(
                 )
 
         def multiply(accs):
-            products = work.tile([P, 2, UNIT_HEADS, PARITY, HEAD_DIM], F32, tag="products")
+            products = work.tile([P, UNIT_HEADS, PARITY, 2 * HEAD_DIM], F32, tag="products")
+            shape = [P, UNIT_HEADS, PAIRS, 2, 2]
             for e in range(PARITY):
                 nc.vector.tensor_tensor(
-                    out=products[:, :, :, e, :],
-                    in0=accs[e][:].unsqueeze(1).to_broadcast([P, 2, UNIT_HEADS, HEAD_DIM]),
-                    in1=factors_by_e[:, :, e]
-                    .unsqueeze(2)
-                    .to_broadcast([P, 2, UNIT_HEADS, HEAD_DIM]),
+                    out=products[:, :, e, :].rearrange("p h (j a u) -> p h j a u", a=2, u=2),
+                    in0=accs[e][:]
+                    .rearrange("p h (j u) -> p h j u", u=2)
+                    .unsqueeze(3)
+                    .to_broadcast(shape),
+                    in1=factors_by_e[:, e].unsqueeze(1).to_broadcast(shape),
                     op=MULT,
                 )
             return products
 
         def add(engine, products, heads, rotated, at=0):
             h0, h1 = heads
-            own = products[:, 0, h0:h1].rearrange("p h e (j r) -> p (h e j) r", r=2)
-            other = products[:, 1, h0:h1].rearrange("p h e (j r) -> p (h e j) r", r=2)
+            both_terms = products[:, h0:h1].rearrange("p h e (c u) -> p (h e c) u", u=2)
             engine.tensor_tensor(
-                out=rotated[:, at : at + h1 - h0].rearrange("p h e (j r) -> p (h e j) r", r=2),
-                in0=own,
-                in1=other[:, :, ::-1],
+                out=rotated[:, at : at + h1 - h0].rearrange("p h e c -> p (h e c)"),
+                in0=both_terms[:, :, 0],
+                in1=both_terms[:, :, 1],
                 op=ADD,
             )
 
@@ -184,10 +185,12 @@ def tile_ropeflashattention_pa_s_kernel(
         first_half, second_half = (0, 2), (2, 4)
 
         whole = (0, UNIT_HEADS)
-        acc_q0 = [project(q0, e) for e in both]
-        acc_v0 = [project(v0, e) for e in both]
+        acc_q0, acc_v0, acc_v4 = [], [], []
+        for e in both:
+            acc_q0.append(project(q0, e))
+            acc_v0.append(project(v0, e))
+            acc_v4.append(project(v4, e))
         acc_q4 = [project(q4, e) for e in both]
-        acc_v4 = [project(v4, e) for e in both]
         prod_q0 = multiply(acc_q0)
         store(sync2, V, 0, copy_out(acc_v0))
         acc_k0 = [project(k0, e) for e in both]
@@ -208,7 +211,7 @@ def tile_ropeflashattention_pa_s_kernel(
         rot_k25 = new_result(4)
         add(nc.vector, prod_k0, second_half, rot_k25, 0)
         add(nc.vector, prod_k4, first_half, rot_k25, 2)
-        store((nc.scalar, nc.sync), K, 2, rot_k25)
+        store(sync2, K, 2, rot_k25)
         rot_k67 = new_result(2)
         add(nc.vector, prod_k4, second_half, rot_k67)
-        store((nc.scalar, nc.sync), K, 6, rot_k67)
+        store(sync2, K, 6, rot_k67)

@@ -101,9 +101,8 @@ def tile_ropeflashattention_pa_s_kernel(
                     x_as_words[:, words_per_row * e + u : words_per_row * (e + 1) : 2],
                     identity[:],
                 )
-            nc.scalar.copy(
-                out=grouped_e[:].bitcast(F32), in_=flipped[:].rearrange("p u m -> p m u")
-            )
+            copier = nc.vector.tensor_copy if e == 0 else nc.scalar.copy
+            copier(out=grouped_e[:].bitcast(F32), in_=flipped[:].rearrange("p u m -> p m u"))
         x_codes = []
         x_scales = []
         for e in range(PARITY):

@@ -25,6 +25,7 @@ UNIT_HEADS = 4
 UNIT_COLS = UNIT_HEADS * HEAD_DIM
 Q, K, V = 0, 1, 2
 WARM_UP = 4
+HOLD = 2
 
 FLOPS = 2 * BATCH * SEQ * MODEL * 3 * MODEL
 
@@ -103,6 +104,9 @@ def tile_ropeflashattention_pa_s_kernel(
                 )
             copier = nc.vector.tensor_copy if e == 0 else nc.scalar.copy
             copier(out=grouped_e[:].bitcast(F32), in_=flipped[:].rearrange("p u m -> p m u"))
+        for hold in range(HOLD):
+            unused = banks.tile([P, P], F32, tag="bank")
+            nc.tensor.matmul(unused[:], lhsT=zeros[:], rhs=zeros[:], start=True, stop=True)
         x_codes = []
         x_scales = []
         for e in range(PARITY):

@@ -171,6 +171,15 @@ def tile_ropeflashattention_pa_s_kernel(
                 op=ADD,
             )
 
+        def add_parity(engine, products, e, rotated):
+            both_terms = products[:, :, e, :].rearrange("p h (c u) -> p h c u", u=2)
+            engine.tensor_tensor(
+                out=rotated[:, :, e, :],
+                in0=both_terms[:, :, :, 0],
+                in1=both_terms[:, :, :, 1],
+                op=ADD,
+            )
+
         def new_result(heads):
             rotated = results.tile([P, heads, PARITY, HEAD_DIM], F32, tag="result")
             return rotated
@@ -199,7 +208,8 @@ def tile_ropeflashattention_pa_s_kernel(
         acc_k0 = [project(k0, e) for e in both]
         store(sync2, V, 4, copy_out(acc_v4))
         rot_q0 = new_result(4)
-        add(nc.gpsimd, prod_q0, whole, rot_q0)
+        for e in both:
+            add_parity(nc.gpsimd, prod_q0, e, rot_q0)
         store(sync2, Q, 0, rot_q0)
         prod_q4 = multiply(acc_q4)
         acc_k4 = [project(k4, e) for e in both]

@@ -226,5 +226,6 @@ def tile_ropeflashattention_pa_s_kernel(
         add(nc.vector, prod_k4, first_half, rot_k25, 2)
         store(sync2, K, 2, rot_k25)
         rot_k67 = new_result(2)
-        add(nc.vector, prod_k4, second_half, rot_k67)
+        add(nc.gpsimd, prod_k4, (3, 4), rot_k67, 1)
+        add(nc.vector, prod_k4, (2, 3), rot_k67, 0)
         store(sync2, K, 6, rot_k67)

@@ -25,7 +25,6 @@ UNIT_HEADS = 4
 UNIT_COLS = UNIT_HEADS * HEAD_DIM
 Q, K, V = 0, 1, 2
 WARM_UP = 4
-HOLD = 2
 
 FLOPS = 2 * BATCH * SEQ * MODEL * 3 * MODEL
 
@@ -79,13 +78,26 @@ def tile_ropeflashattention_pa_s_kernel(
 
         identity = keep.tile([P, P], F32)
         make_identity(nc, identity[:])
+        exchange = keep.tile([P, PAIRS * 2, 2], F32)
+        by_pair = identity[:].rearrange("p (c u) -> p c u", u=2)
+        for u in range(2):
+            nc.gpsimd.tensor_copy(out=exchange[:, :, u], in_=by_pair[:, :, 1 - u])
 
-        factors = keep.tile([P, PARITY * PAIRS, 4], BF16)
-        nc.vector.tensor_copy(
-            out=factors[:, :, 0:4:3],
-            in_=cos_sb[:].unsqueeze(2).to_broadcast([P, PARITY * PAIRS, 2]),
+        spread = keep.tile([P, 2, PARITY, 2, PAIRS, 2], F32)
+        cos_spread, sin_spread = [
+            table_sb[:]
+            .rearrange("p (e j) -> p e j", e=PARITY)
+            .unsqueeze(2)
+            .to_broadcast([P, PARITY, 2, PAIRS])
+            for table_sb in (cos_sb, sin_sb)
+        ]
+        nc.scalar.copy(out=spread[:, 1, :, :, :, 0], in_=sin_spread)
+        nc.gpsimd.tensor_scalar(
+            out=spread[:, 1, :, :, :, 1], in0=sin_spread, scalar1=-1.0, scalar2=0.0, op0=MULT, op1=ADD
         )
-        nc.vector.tensor_scalar_mul(out=factors[:, :, 1], in0=sin_sb[:], scalar1=-1.0)
+        for u in range(2):
+            nc.vector.tensor_copy(out=spread[:, 0, :, :, :, u], in_=cos_spread)
+        factors = keep.tile([P, PARITY * PAIRS, 4], BF16)
         nc.vector.tensor_copy(out=factors[:, :, 2], in_=sin_sb[:])
         factors_by_e = factors[:].rearrange("p (e j) (a u) -> p e j a u", e=PARITY, u=2)
 
@@ -104,31 +116,50 @@ def tile_ropeflashattention_pa_s_kernel(
                 )
             copier = nc.vector.tensor_copy if e == 0 else nc.scalar.copy
             copier(out=grouped_e[:].bitcast(F32), in_=flipped[:].rearrange("p u m -> p m u"))
-        for hold in range(HOLD):
-            unused = banks.tile([P, P], F32, tag="bank")
-            nc.tensor.matmul(unused[:], lhsT=zeros[:], rhs=zeros[:], start=True, stop=True)
-        x_codes = []
-        x_scales = []
-        for e in range(PARITY):
-            codes_e = keep.tile([P, P], U32, align_bytes=64, name="x_codes%d" % e)
-            scales_e = keep.tile([P, P], U8, align_bytes=64, name="x_scales%d" % e)
+        nc.vector.tensor_scalar_mul(out=factors[:, :, 1], in0=sin_sb[:], scalar1=-1.0)
+        table_bank = banks.tile([P, 2, PARITY, P], F32, tag="bank")
+        for w in (1, 0):
+            for e in range(PARITY):
+                nc.tensor.transpose(
+                    table_bank[:, w, e, :],
+                    spread[:, w, e].rearrange("p g j u -> p (g j u)"),
+                    identity[:],
+                )
+        tables_t = keep.tile([P, 2, PARITY * P], BF16)
+        nc.scalar.copy(
+            out=tables_t[:].rearrange("p w t -> p (w t)"),
+            in_=table_bank[:].rearrange("p w e t -> p (w e t)"),
+        )
+        x_codes = keep.tile([P, PARITY * P], U32, align_bytes=64)
+        x_scales = keep.tile([P, PARITY * P], U8, align_bytes=64)
+
+        def quantise(e):
             nc.vector.quantize_mx(
-                out=codes_e[:].bitcast(FP8X4),
-                scales=scales_e[:],
+                out=x_codes[:, P * e : P * (e + 1)].bitcast(FP8X4),
+                scales=x_scales[:, P * e : P * (e + 1)],
                 in_=grouped[e][:].rearrange("p m t -> p (m t)"),
             )
-            x_codes.append(codes_e)
-            x_scales.append(scales_e)
 
-        def project(unit, e):
+        quantise(0)
+        nc.vector.tensor_copy(
+            out=factors[:, :, 0:4:3],
+            in_=cos_sb[:].unsqueeze(2).to_broadcast([P, PARITY * PAIRS, 2]),
+        )
+        quantise(1)
+
+        def new_bank():
+            bank = banks.tile([P, PARITY, UNIT_COLS], F32, tag="bank")
+            return bank
+
+        def project(unit, e, bank=None, half=0):
             which, first_head = unit
             head_col = first_head * HEAD_DIM
             first_col = which * MODEL + head_col
-            acc = banks.tile([P, UNIT_HEADS, HEAD_DIM], F32, tag="bank")
+            acc = new_bank() if bank is None else bank
             nc.tensor.matmul_mx(
-                out=acc[:].rearrange("p h d -> p (h d)"),
-                lhsT=x_codes[e][:].bitcast(FP8X4),
-                lhsT_scale=x_scales[e][:],
+                out=acc[:, half, :],
+                lhsT=x_codes[:, P * e : P * (e + 1)].bitcast(FP8X4),
+                lhsT_scale=x_scales[:, P * e : P * (e + 1)],
                 rhs=w_words[:, which, 2 * head_col : 2 * (head_col + UNIT_COLS)].bitcast(FP4X4),
                 rhs_scale=w_scales[:, first_col : first_col + UNIT_COLS],
                 start=True,
@@ -146,29 +177,19 @@ def tile_ropeflashattention_pa_s_kernel(
                     in_=result[b:P:BATCH].rearrange("p h e d -> p h (e d)"),
                 )
 
-        def multiply(accs):
+        def new_products():
             products = work.tile([P, UNIT_HEADS, PARITY, 2 * HEAD_DIM], F32, tag="products")
-            shape = [P, UNIT_HEADS, PAIRS, 2, 2]
-            for e in range(PARITY):
-                nc.vector.tensor_tensor(
-                    out=products[:, :, e, :].rearrange("p h (j a u) -> p h j a u", a=2, u=2),
-                    in0=accs[e][:]
-                    .rearrange("p h (j u) -> p h j u", u=2)
-                    .unsqueeze(3)
-                    .to_broadcast(shape),
-                    in1=factors_by_e[:, e].unsqueeze(1).to_broadcast(shape),
-                    op=MULT,
-                )
             return products
 
-        def add(engine, products, heads, rotated, at=0):
-            h0, h1 = heads
-            both_terms = products[:, h0:h1].rearrange("p h e (c u) -> p (h e c) u", u=2)
+        def multiply(engine, sums, e, products):
+            shape = [P, UNIT_HEADS, PAIRS, 2, 2]
             engine.tensor_tensor(
-                out=rotated[:, at : at + h1 - h0].rearrange("p h e c -> p (h e c)"),
-                in0=both_terms[:, :, 0],
-                in1=both_terms[:, :, 1],
-                op=ADD,
+                out=products[:, :, e, :].rearrange("p h (j a u) -> p h j a u", a=2, u=2),
+                in0=sums.rearrange("p (h j u) -> p h j u", h=UNIT_HEADS, u=2)
+                .unsqueeze(3)
+                .to_broadcast(shape),
+                in1=factors_by_e[:, e].unsqueeze(1).to_broadcast(shape),
+                op=MULT,
             )
 
         def add_parity(engine, products, e, rotated):
@@ -187,45 +208,106 @@ def tile_ropeflashattention_pa_s_kernel(
         def copy_out(accs):
             copied = results.tile([P, UNIT_HEADS, PARITY, HEAD_DIM], F32, tag="result")
             for e in range(PARITY):
-                nc.scalar.copy(out=copied[:, :, e, :], in_=accs[e][:])
+                nc.scalar.copy(
+                    out=copied[:, :, e, :],
+                    in_=accs[e][:, 0, :].rearrange("p (h d) -> p h d", h=UNIT_HEADS),
+                )
             return copied
+
+        def copy_out_bank(bank):
+            copied = results.tile([P, UNIT_HEADS, PARITY, HEAD_DIM], F32, tag="result")
+            nc.scalar.copy(
+                out=copied[:].rearrange("p h e d -> p e h d"),
+                in_=bank[:].rearrange("p e (h d) -> p e h d", h=UNIT_HEADS),
+            )
+            return copied
+
+        def project_turned(unit):
+            which, first_head = unit
+            head_col = first_head * HEAD_DIM
+            first_col = which * MODEL + head_col
+            acc = new_bank()
+            for pair in range(2):
+                nc.tensor.matmul_mx(
+                    out=acc[:, pair, :],
+                    lhsT=w_words[:, which, 2 * (head_col + P * pair) : 2 * (head_col + P * (pair + 1))].bitcast(FP4X4),
+                    lhsT_scale=w_scales[:, first_col + P * pair : first_col + P * (pair + 1)],
+                    rhs=x_codes[:].bitcast(FP8X4),
+                    rhs_scale=x_scales[:],
+                    start=True,
+                    stop=True,
+                )
+            return acc
+
+        def multiply_turned(acc):
+            products = []
+            for pair in range(2):
+                prod_t = work.tile([P, 2, PARITY * P], F32, tag="prod_t")
+                nc.vector.tensor_tensor(
+                    out=prod_t[:],
+                    in0=acc[:, pair, :].unsqueeze(1).to_broadcast([P, 2, PARITY * P]),
+                    in1=tables_t[:],
+                    op=MULT,
+                )
+                products.append(prod_t)
+            return products
+
+        def turn_back(products, rotated):
+            for pair in range(2):
+                summed = banks.tile([P, PARITY, 2, HEAD_DIM], F32, tag="bank")
+                for e in both:
+                    for w, order in ((0, identity[:]), (1, exchange[:].rearrange("p c u -> p (c u)"))):
+                        nc.tensor.matmul(
+                            summed[:, e].rearrange("p g d -> p (g d)"),
+                            lhsT=products[pair][:, w, P * e : P * (e + 1)],
+                            rhs=order,
+                            start=w == 0,
+                            stop=w == 1,
+                            is_transpose=True,
+                        )
+                nc.scalar.copy(
+                    out=rotated[pair].rearrange("p g e d -> p e g d"), in_=summed[:]
+                )
 
         both = range(PARITY)
         q0, q4, k0, k4, v0, v4 = (Q, 0), (Q, 4), (K, 0), (K, 4), (V, 0), (V, 4)
 
         sync2 = (nc.sync, nc.sync)
-        first_half, second_half = (0, 2), (2, 4)
-
-        whole = (0, UNIT_HEADS)
-        acc_q0, acc_v0, acc_v4 = [], [], []
+        acc_q0, acc_v0 = [], []
+        bank_v4 = None
         for e in both:
             acc_q0.append(project(q0, e))
             acc_v0.append(project(v0, e))
-            acc_v4.append(project(v4, e))
-        acc_q4 = [project(q4, e) for e in both]
-        prod_q0 = multiply(acc_q0)
+            bank_v4 = project(v4, e, bank_v4, e)
+        acc_q4 = project_turned(q4)
+        acc_k0 = project_turned(k0)
+        acc_k4 = [project(k4, e) for e in both]
+
+        prod_q0 = new_products()
+        for e in both:
+            multiply(nc.vector, acc_q0[e][:, 0, :], e, prod_q0)
         store(sync2, V, 0, copy_out(acc_v0))
-        acc_k0 = [project(k0, e) for e in both]
-        store(sync2, V, 4, copy_out(acc_v4))
+        store(sync2, V, 4, copy_out_bank(bank_v4))
+        sums_k4 = keep.tile([P, UNIT_COLS], F32)
+        nc.scalar.copy(out=sums_k4[:], in_=acc_k4[0][:, 0, :])
         rot_q0 = new_result(4)
         for e in both:
             add_parity(nc.gpsimd, prod_q0, e, rot_q0)
         store(sync2, Q, 0, rot_q0)
-        prod_q4 = multiply(acc_q4)
-        acc_k4 = [project(k4, e) for e in both]
+
         rot_q4 = new_result(4)
-        add(nc.gpsimd, prod_q4, whole, rot_q4)
+        turn_back(multiply_turned(acc_q4), [rot_q4[:, 0:2], rot_q4[:, 2:4]])
         store(sync2, Q, 4, rot_q4)
-        prod_k0 = multiply(acc_k0)
-        rot_k01 = new_result(2)
-        add(nc.gpsimd, prod_k0, first_half, rot_k01)
-        store(sync2, K, 0, rot_k01)
-        prod_k4 = multiply(acc_k4)
-        rot_k25 = new_result(4)
-        add(nc.vector, prod_k0, second_half, rot_k25, 0)
-        add(nc.vector, prod_k4, first_half, rot_k25, 2)
-        store(sync2, K, 2, rot_k25)
-        rot_k67 = new_result(2)
-        add(nc.gpsimd, prod_k4, (3, 4), rot_k67, 1)
-        add(nc.vector, prod_k4, (2, 3), rot_k67, 0)
-        store(sync2, K, 6, rot_k67)
+
+        prod_k4 = new_products()
+        multiply(nc.gpsimd, sums_k4[:], 0, prod_k4)
+        rot_k0, rot_k2 = new_result(2), new_result(2)
+        turn_back(multiply_turned(acc_k0), [rot_k0[:], rot_k2[:]])
+        store(sync2, K, 0, rot_k0)
+
+        multiply(nc.vector, acc_k4[1][:, 0, :], 1, prod_k4)
+        rot_k4 = new_result(4)
+        add_parity(nc.vector, prod_k4, 1, rot_k4)
+        add_parity(nc.gpsimd, prod_k4, 0, rot_k4)
+        store(sync2, K, 4, rot_k4)
+        store(sync2, K, 2, rot_k2)

@@ -95,10 +95,11 @@ def tile_ropeflashattention_pa_s_kernel(
         nc.gpsimd.tensor_scalar(
             out=spread[:, 1, :, :, :, 1], in0=sin_spread, scalar1=-1.0, scalar2=0.0, op0=MULT, op1=ADD
         )
-        for u in range(2):
-            nc.vector.tensor_copy(out=spread[:, 0, :, :, :, u], in_=cos_spread)
+        nc.vector.tensor_copy(
+            out=spread[:, 0],
+            in_=cos_spread.unsqueeze(4).to_broadcast([P, PARITY, 2, PAIRS, 2]),
+        )
         factors = keep.tile([P, PARITY * PAIRS, 4], BF16)
-        nc.vector.tensor_copy(out=factors[:, :, 2], in_=sin_sb[:])
         factors_by_e = factors[:].rearrange("p (e j) (a u) -> p e j a u", e=PARITY, u=2)
 
         x_as_words = x_sb[:].bitcast(F32)
@@ -116,7 +117,7 @@ def tile_ropeflashattention_pa_s_kernel(
                 )
             copier = nc.vector.tensor_copy if e == 0 else nc.scalar.copy
             copier(out=grouped_e[:].bitcast(F32), in_=flipped[:].rearrange("p u m -> p m u"))
-        nc.vector.tensor_scalar_mul(out=factors[:, :, 1], in0=sin_sb[:], scalar1=-1.0)
+        nc.vector.tensor_copy(out=factors[:, :, 2], in_=sin_sb[:])
         table_bank = banks.tile([P, 2, PARITY, P], F32, tag="bank")
         for w in (1, 0):
             for e in range(PARITY):
@@ -141,6 +142,7 @@ def tile_ropeflashattention_pa_s_kernel(
             )
 
         quantise(0)
+        nc.vector.tensor_scalar_mul(out=factors[:, :, 1], in0=sin_sb[:], scalar1=-1.0)
         nc.vector.tensor_copy(
             out=factors[:, :, 0:4:3],
             in_=cos_sb[:].unsqueeze(2).to_broadcast([P, PARITY * PAIRS, 2]),
@@ -307,7 +309,7 @@ def tile_ropeflashattention_pa_s_kernel(
 
         multiply(nc.vector, acc_k4[1][:, 0, :], 1, prod_k4)
         rot_k4 = new_result(4)
-        add_parity(nc.vector, prod_k4, 1, rot_k4)
-        add_parity(nc.gpsimd, prod_k4, 0, rot_k4)
+        for e in both:
+            add_parity(nc.vector, prod_k4, e, rot_k4)
         store(sync2, K, 4, rot_k4)
         store(sync2, K, 2, rot_k2)

@@ -126,11 +126,12 @@ def tile_ropeflashattention_pa_s_kernel(
                     spread[:, w, e].rearrange("p g j u -> p (g j u)"),
                     identity[:],
                 )
-        tables_t = keep.tile([P, 2, PARITY * P], BF16)
-        nc.scalar.copy(
-            out=tables_t[:].rearrange("p w t -> p (w t)"),
-            in_=table_bank[:].rearrange("p w e t -> p (w e t)"),
-        )
+        tables_t = keep.tile([P, 2, 2, P // 2, BATCH], BF16)
+        for w in range(2):
+            nc.scalar.copy(
+                out=tables_t[:, w],
+                in_=table_bank[:, w].rearrange("p e (i r b) -> p r (e i) b", r=2, b=BATCH),
+            )
         x_codes = keep.tile([P, PARITY * P], U32, align_bytes=64)
         x_scales = keep.tile([P, PARITY * P], U8, align_bytes=64)
 
@@ -242,34 +243,50 @@ def tile_ropeflashattention_pa_s_kernel(
             return acc
 
         def multiply_turned(acc):
+            sums = acc[:].rearrange("p g (e i r b) -> p r (e i) g b", e=PARITY, r=2, b=BATCH)
             products = []
-            for pair in range(2):
-                prod_t = work.tile([P, 2, PARITY * P], F32, tag="prod_t")
-                nc.vector.tensor_tensor(
-                    out=prod_t[:],
-                    in0=acc[:, pair, :].unsqueeze(1).to_broadcast([P, 2, PARITY * P]),
-                    in1=tables_t[:],
-                    op=MULT,
-                )
+            for r in range(2):
+                prod_t = work.tile([P, 2, P // 2, 2, BATCH], F32, tag="prod_t")
+                for w in range(2):
+                    nc.vector.tensor_tensor(
+                        out=prod_t[:, w],
+                        in0=sums[:, r],
+                        in1=tables_t[:, w, r].unsqueeze(2).to_broadcast([P, P // 2, 2, BATCH]),
+                        op=MULT,
+                    )
                 products.append(prod_t)
             return products
 
         def turn_back(products, rotated):
-            for pair in range(2):
+            for r in range(2):
+                columns = products[r][:].rearrange("p w (e i) g b -> p w e (i g b)", e=PARITY)
                 summed = banks.tile([P, PARITY, 2, HEAD_DIM], F32, tag="bank")
                 for e in both:
                     for w, order in ((0, identity[:]), (1, exchange[:].rearrange("p c u -> p (c u)"))):
                         nc.tensor.matmul(
                             summed[:, e].rearrange("p g d -> p (g d)"),
-                            lhsT=products[pair][:, w, P * e : P * (e + 1)],
+                            lhsT=columns[:, w, e],
                             rhs=order,
                             start=w == 0,
                             stop=w == 1,
                             is_transpose=True,
                         )
                 nc.scalar.copy(
-                    out=rotated[pair].rearrange("p g e d -> p e g d"), in_=summed[:]
+                    out=rotated[:, :, r].rearrange("p g e d -> p e g d"), in_=summed[:]
                 )
+
+        def store_turned(which, first_head, rotated):
+            for b in range(BATCH):
+                nc.sync.dma_start(
+                    out=outputs[which][b, first_head : first_head + UNIT_HEADS].rearrange(
+                        "h (i t) d -> i h (t d)", t=2 * PARITY
+                    ),
+                    in_=rotated[b:P:BATCH].rearrange("p g r e d -> p g (r e d)"),
+                )
+
+        def new_turned():
+            rotated = results.tile([P, 2, 2, PARITY, HEAD_DIM], F32, tag="turned")
+            return rotated
 
         both = range(PARITY)
         q0, q4, k0, k4, v0, v4 = (Q, 0), (Q, 4), (K, 0), (K, 4), (V, 0), (V, 4)
@@ -297,19 +314,18 @@ def tile_ropeflashattention_pa_s_kernel(
             add_parity(nc.gpsimd, prod_q0, e, rot_q0)
         store(sync2, Q, 0, rot_q0)
 
-        rot_q4 = new_result(4)
-        turn_back(multiply_turned(acc_q4), [rot_q4[:, 0:2], rot_q4[:, 2:4]])
-        store(sync2, Q, 4, rot_q4)
+        rot_q4 = new_turned()
+        turn_back(multiply_turned(acc_q4), rot_q4)
+        store_turned(Q, 4, rot_q4)
 
         prod_k4 = new_products()
         multiply(nc.gpsimd, sums_k4[:], 0, prod_k4)
-        rot_k0, rot_k2 = new_result(2), new_result(2)
-        turn_back(multiply_turned(acc_k0), [rot_k0[:], rot_k2[:]])
-        store(sync2, K, 0, rot_k0)
+        rot_k0 = new_turned()
+        turn_back(multiply_turned(acc_k0), rot_k0)
 
         multiply(nc.vector, acc_k4[1][:, 0, :], 1, prod_k4)
         rot_k4 = new_result(4)
         for e in both:
             add_parity(nc.vector, prod_k4, e, rot_k4)
         store(sync2, K, 4, rot_k4)
-        store(sync2, K, 2, rot_k2)
+        store_turned(K, 0, rot_k0)

@@ -25,6 +25,7 @@ UNIT_HEADS = 4
 UNIT_COLS = UNIT_HEADS * HEAD_DIM
 Q, K, V = 0, 1, 2
 WARM_UP = 4
+POOL_HEADS = 3
 
 FLOPS = 2 * BATCH * SEQ * MODEL * 3 * MODEL
 
@@ -38,8 +39,12 @@ def tile_ropeflashattention_pa_s_kernel(
     with tc.tile_pool(name="keep", bufs=1) as keep, tc.tile_pool(
         name="work", bufs=4
     ) as work, tc.tile_pool(name="results", bufs=9) as results, tc.psum_pool(
-        name="banks", bufs=8
+        name="banks", bufs=1
     ) as banks, tc.manual_schedule():
+        def new_tile_in_bank(bank, shape):
+            in_bank = banks.tile([P] + shape, F32, tag="bank%d" % bank)
+            return in_bank
+
         x_sb = keep.tile([P, PARITY * MODEL], BF16)
         nc.sync.dma_start(
             out=x_sb[:], in_=x.rearrange("b (i e) k -> i b (e k)", e=PARITY)
@@ -73,7 +78,7 @@ def tile_ropeflashattention_pa_s_kernel(
         zeros = keep.tile([P, P], F32)
         nc.gpsimd.memset(zeros[:], 0.0)
         for warm in range(WARM_UP):
-            unused = banks.tile([P, P], F32, tag="bank")
+            unused = new_tile_in_bank(warm, [P])
             nc.tensor.matmul(unused[:], lhsT=zeros[:], rhs=zeros[:], start=True, stop=True)
 
         identity = keep.tile([P, P], F32)
@@ -108,7 +113,7 @@ def tile_ropeflashattention_pa_s_kernel(
         for e in range(PARITY):
             grouped_e = keep.tile([P, P, PACK], BF16, align_bytes=64, name="grouped%d" % e)
             grouped.append(grouped_e)
-            flipped = banks.tile([P, 2, P], F32, tag="bank")
+            flipped = new_tile_in_bank(4 + e, [2, P])
             for u in range(2):
                 nc.tensor.transpose(
                     flipped[:, u, :],
@@ -118,7 +123,7 @@ def tile_ropeflashattention_pa_s_kernel(
             copier = nc.vector.tensor_copy if e == 0 else nc.scalar.copy
             copier(out=grouped_e[:].bitcast(F32), in_=flipped[:].rearrange("p u m -> p m u"))
         nc.vector.tensor_copy(out=factors[:, :, 2], in_=sin_sb[:])
-        table_bank = banks.tile([P, 2, PARITY, P], F32, tag="bank")
+        table_bank = new_tile_in_bank(6, [2, PARITY, P])
         for w in (1, 0):
             for e in range(PARITY):
                 nc.tensor.transpose(
@@ -150,15 +155,10 @@ def tile_ropeflashattention_pa_s_kernel(
         )
         quantise(1)
 
-        def new_bank():
-            bank = banks.tile([P, PARITY, UNIT_COLS], F32, tag="bank")
-            return bank
-
-        def project(unit, e, bank=None, half=0):
+        def project(unit, e, acc, half=0):
             which, first_head = unit
             head_col = first_head * HEAD_DIM
             first_col = which * MODEL + head_col
-            acc = new_bank() if bank is None else bank
             nc.tensor.matmul_mx(
                 out=acc[:, half, :],
                 lhsT=x_codes[:, P * e : P * (e + 1)].bitcast(FP8X4),
@@ -185,10 +185,11 @@ def tile_ropeflashattention_pa_s_kernel(
             return products
 
         def multiply(engine, sums, e, products):
-            shape = [P, UNIT_HEADS, PAIRS, 2, 2]
+            heads = products.shape[1]
+            shape = [P, heads, PAIRS, 2, 2]
             engine.tensor_tensor(
                 out=products[:, :, e, :].rearrange("p h (j a u) -> p h j a u", a=2, u=2),
-                in0=sums.rearrange("p (h j u) -> p h j u", h=UNIT_HEADS, u=2)
+                in0=sums.rearrange("p (h j u) -> p h j u", h=heads, u=2)
                 .unsqueeze(3)
                 .to_broadcast(shape),
                 in1=factors_by_e[:, e].unsqueeze(1).to_broadcast(shape),
@@ -225,11 +226,10 @@ def tile_ropeflashattention_pa_s_kernel(
             )
             return copied
 
-        def project_turned(unit):
+        def project_turned(unit, acc):
             which, first_head = unit
             head_col = first_head * HEAD_DIM
             first_col = which * MODEL + head_col
-            acc = new_bank()
             for pair in range(2):
                 nc.tensor.matmul_mx(
                     out=acc[:, pair, :],
@@ -248,32 +248,38 @@ def tile_ropeflashattention_pa_s_kernel(
             for r in range(2):
                 prod_t = work.tile([P, 2, P // 2, 2, BATCH], F32, tag="prod_t")
                 for w in range(2):
-                    nc.vector.tensor_tensor(
-                        out=prod_t[:, w],
-                        in0=sums[:, r],
-                        in1=tables_t[:, w, r].unsqueeze(2).to_broadcast([P, P // 2, 2, BATCH]),
-                        op=MULT,
-                    )
+                    parts = PARITY if r and w else 1
+                    part = P // 2 // parts
+                    for first in range(0, P // 2, part):
+                        nc.vector.tensor_tensor(
+                            out=prod_t[:, w, first : first + part],
+                            in0=sums[:, r, first : first + part],
+                            in1=tables_t[:, w, r, first : first + part]
+                            .unsqueeze(2)
+                            .to_broadcast([P, part, 2, BATCH]),
+                            op=MULT,
+                        )
                 products.append(prod_t)
             return products
 
         def turn_back(products, rotated):
             for r in range(2):
                 columns = products[r][:].rearrange("p w (e i) g b -> p w e (i g b)", e=PARITY)
-                summed = banks.tile([P, PARITY, 2, HEAD_DIM], F32, tag="bank")
+                summed = []
                 for e in both:
-                    for w, order in ((0, identity[:]), (1, exchange[:].rearrange("p c u -> p (c u)"))):
+                    summed.append(new_tile_in_bank(2 * r + e, [2, HEAD_DIM]))
+                for w, order in ((0, identity[:]), (1, exchange[:].rearrange("p c u -> p (c u)"))):
+                    for e in both:
                         nc.tensor.matmul(
-                            summed[:, e].rearrange("p g d -> p (g d)"),
+                            summed[e][:].rearrange("p g d -> p (g d)"),
                             lhsT=columns[:, w, e],
                             rhs=order,
                             start=w == 0,
                             stop=w == 1,
                             is_transpose=True,
                         )
-                nc.scalar.copy(
-                    out=rotated[:, :, r].rearrange("p g e d -> p e g d"), in_=summed[:]
-                )
+                for e in both:
+                    nc.scalar.copy(out=rotated[:, :, r, e], in_=summed[e][:])
 
         def store_turned(which, first_head, rotated):
             for b in range(BATCH):
@@ -292,23 +298,25 @@ def tile_ropeflashattention_pa_s_kernel(
         q0, q4, k0, k4, v0, v4 = (Q, 0), (Q, 4), (K, 0), (K, 4), (V, 0), (V, 4)
 
         sync2 = (nc.sync, nc.sync)
-        acc_q0, acc_v0 = [], []
-        bank_v4 = None
+        sums_shape = [PARITY, UNIT_COLS]
+        acc_q0 = [new_tile_in_bank(bank, sums_shape) for bank in (7, 2)]
+        acc_v0 = [new_tile_in_bank(bank, sums_shape) for bank in (0, 3)]
+        bank_v4 = new_tile_in_bank(1, sums_shape)
         for e in both:
-            acc_q0.append(project(q0, e))
-            acc_v0.append(project(v0, e))
-            bank_v4 = project(v4, e, bank_v4, e)
-        acc_q4 = project_turned(q4)
-        acc_k0 = project_turned(k0)
-        acc_k4 = [project(k4, e) for e in both]
+            project(q0, e, acc_q0[e])
+            project(v0, e, acc_v0[e])
+            project(v4, e, bank_v4, e)
+        acc_q4 = project_turned(q4, new_tile_in_bank(4, sums_shape))
+        acc_k0 = project_turned(k0, new_tile_in_bank(5, sums_shape))
+        acc_k4 = [project(k4, e, new_tile_in_bank(6 + e, sums_shape)) for e in both]
 
         prod_q0 = new_products()
         for e in both:
-            multiply(nc.vector, acc_q0[e][:, 0, :], e, prod_q0)
+            multiply(nc.vector, acc_q0[e][:, 0, :], e, prod_q0[:])
         store(sync2, V, 0, copy_out(acc_v0))
         store(sync2, V, 4, copy_out_bank(bank_v4))
-        sums_k4 = keep.tile([P, UNIT_COLS], F32)
-        nc.scalar.copy(out=sums_k4[:], in_=acc_k4[0][:, 0, :])
+        sums_k4 = keep.tile([P, POOL_HEADS * HEAD_DIM], F32)
+        nc.scalar.copy(out=sums_k4[:], in_=acc_k4[0][:, 0, 0 : POOL_HEADS * HEAD_DIM])
         rot_q0 = new_result(4)
         for e in both:
             add_parity(nc.gpsimd, prod_q0, e, rot_q0)
@@ -319,13 +327,16 @@ def tile_ropeflashattention_pa_s_kernel(
         store_turned(Q, 4, rot_q4)
 
         prod_k4 = new_products()
-        multiply(nc.gpsimd, sums_k4[:], 0, prod_k4)
+        multiply(nc.gpsimd, sums_k4[:], 0, prod_k4[:, 0:POOL_HEADS])
         rot_k0 = new_turned()
         turn_back(multiply_turned(acc_k0), rot_k0)
 
-        multiply(nc.vector, acc_k4[1][:, 0, :], 1, prod_k4)
+        multiply(
+            nc.vector, acc_k4[0][:, 0, POOL_HEADS * HEAD_DIM :], 0, prod_k4[:, POOL_HEADS:]
+        )
+        multiply(nc.vector, acc_k4[1][:, 0, :], 1, prod_k4[:])
         rot_k4 = new_result(4)
         for e in both:
             add_parity(nc.vector, prod_k4, e, rot_k4)
-        store(sync2, K, 4, rot_k4)
         store_turned(K, 0, rot_k0)
+        store(sync2, K, 4, rot_k4)

@@ -124,7 +124,7 @@ def tile_ropeflashattention_pa_s_kernel(
             copier(out=grouped_e[:].bitcast(F32), in_=flipped[:].rearrange("p u m -> p m u"))
         nc.vector.tensor_copy(out=factors[:, :, 2], in_=sin_sb[:])
         table_bank = new_tile_in_bank(6, [2, PARITY, P])
-        for w in (1, 0):
+        for w in range(2):
             for e in range(PARITY):
                 nc.tensor.transpose(
                     table_bank[:, w, e, :],
@@ -209,14 +209,13 @@ def tile_ropeflashattention_pa_s_kernel(
             rotated = results.tile([P, heads, PARITY, HEAD_DIM], F32, tag="result")
             return rotated
 
-        def copy_out(accs):
-            copied = results.tile([P, UNIT_HEADS, PARITY, HEAD_DIM], F32, tag="result")
+        def copy_out_in_halves(accs):
+            halves = [new_result(2), new_result(2)]
             for e in range(PARITY):
-                nc.scalar.copy(
-                    out=copied[:, :, e, :],
-                    in_=accs[e][:, 0, :].rearrange("p (h d) -> p h d", h=UNIT_HEADS),
-                )
-            return copied
+                heads = accs[e][:, 0, :].rearrange("p (h d) -> p h d", h=UNIT_HEADS)
+                for part, copied in enumerate(halves):
+                    nc.scalar.copy(out=copied[:, :, e, :], in_=heads[:, 2 * part : 2 * part + 2])
+            return halves
 
         def copy_out_bank(bank):
             copied = results.tile([P, UNIT_HEADS, PARITY, HEAD_DIM], F32, tag="result")
@@ -302,10 +301,12 @@ def tile_ropeflashattention_pa_s_kernel(
         acc_q0 = [new_tile_in_bank(bank, sums_shape) for bank in (7, 2)]
         acc_v0 = [new_tile_in_bank(bank, sums_shape) for bank in (0, 3)]
         bank_v4 = new_tile_in_bank(1, sums_shape)
-        for e in both:
-            project(q0, e, acc_q0[e])
-            project(v0, e, acc_v0[e])
-            project(v4, e, bank_v4, e)
+        project(q0, 0, acc_q0[0])
+        project(v0, 0, acc_v0[0])
+        project(v4, 0, bank_v4, 0)
+        project(v0, 1, acc_v0[1])
+        project(q0, 1, acc_q0[1])
+        project(v4, 1, bank_v4, 1)
         acc_q4 = project_turned(q4, new_tile_in_bank(4, sums_shape))
         acc_k0 = project_turned(k0, new_tile_in_bank(5, sums_shape))
         acc_k4 = [project(k4, e, new_tile_in_bank(6 + e, sums_shape)) for e in both]
@@ -313,7 +314,8 @@ def tile_ropeflashattention_pa_s_kernel(
         prod_q0 = new_products()
         for e in both:
             multiply(nc.vector, acc_q0[e][:, 0, :], e, prod_q0[:])
-        store(sync2, V, 0, copy_out(acc_v0))
+        for part, half in enumerate(copy_out_in_halves(acc_v0)):
+            store(sync2, V, 2 * part, half)
         store(sync2, V, 4, copy_out_bank(bank_v4))
         sums_k4 = keep.tile([P, POOL_HEADS * HEAD_DIM], F32)
         nc.scalar.copy(out=sums_k4[:], in_=acc_k4[0][:, 0, 0 : POOL_HEADS * HEAD_DIM])
@@ -334,9 +336,13 @@ def tile_ropeflashattention_pa_s_kernel(
         multiply(
             nc.vector, acc_k4[0][:, 0, POOL_HEADS * HEAD_DIM :], 0, prod_k4[:, POOL_HEADS:]
         )
-        multiply(nc.vector, acc_k4[1][:, 0, :], 1, prod_k4[:])
         rot_k4 = new_result(4)
-        for e in both:
-            add_parity(nc.vector, prod_k4, e, rot_k4)
+        pairs_of_heads = (slice(0, 2), slice(2, 4))
+        sums_k4_odd = acc_k4[1][:, 0, :].rearrange("p (g c) -> p g c", g=2)
+        for g, heads in enumerate(pairs_of_heads):
+            multiply(nc.vector, sums_k4_odd[:, g], 1, prod_k4[:, heads])
+        add_parity(nc.vector, prod_k4, 0, rot_k4)
+        for heads in pairs_of_heads:
+            add_parity(nc.vector, prod_k4[:, heads], 1, rot_k4[:, heads])
         store_turned(K, 0, rot_k0)
         store(sync2, K, 4, rot_k4)

import concourse.mybir as mybir
from concourse.masks import make_identity

F32 = mybir.dt.float32
BF16 = mybir.dt.bfloat16
I32 = mybir.dt.int32
U8 = mybir.dt.uint8
U32 = mybir.dt.uint32
FP8X4 = mybir.dt.float8_e4m3fn_x4
FP4X4 = mybir.dt.float4_e2m1fn_x4
MULT = mybir.AluOpType.mult
ADD = mybir.AluOpType.add

P = 128
BATCH = 2
SEQ = 128
HEADS = 8
HEAD_DIM = 64
PAIRS = HEAD_DIM // 2
MODEL = HEADS * HEAD_DIM
PACK = 4
PARITY = 2
ROWS = SEQ // PARITY
UNIT_HEADS = 4
UNIT_COLS = UNIT_HEADS * HEAD_DIM
Q, K, V = 0, 1, 2
WARM_UP = 4
POOL_HEADS = 3

FLOPS = 2 * BATCH * SEQ * MODEL * 3 * MODEL


def tile_ropeflashattention_pa_s_kernel(
    tc, x, w_qkv_words, w_qkv_scales, cos, sin, out_0, out_1, out_2
):
    nc = tc.nc
    outputs = (out_0, out_1, out_2)

    with tc.tile_pool(name="keep", bufs=1) as keep, tc.tile_pool(
        name="work", bufs=4
    ) as work, tc.tile_pool(name="results", bufs=9) as results, tc.psum_pool(
        name="banks", bufs=1
    ) as banks, tc.manual_schedule():
        def new_tile_in_bank(bank, shape):
            in_bank = banks.tile([P] + shape, F32, tag="bank%d" % bank)
            return in_bank

        x_sb = keep.tile([P, PARITY * MODEL], BF16)
        nc.sync.dma_start(
            out=x_sb[:], in_=x.rearrange("b (i e) k -> i b (e k)", e=PARITY)
        )
        cos_sb = keep.tile([P, PARITY * PAIRS], BF16)
        sin_sb = keep.tile([P, PARITY * PAIRS], BF16)
        for table_sb, table in ((cos_sb, cos), (sin_sb, sin)):
            nc.sync.dma_start(
                out=table_sb[:],
                in_=table.rearrange("(i e) j -> i (e j)", e=PARITY)
                .unsqueeze(1)
                .to_broadcast([ROWS, BATCH, PARITY * PAIRS]),
            )
        w_words = keep.tile([P, 3, 2 * MODEL], U8, align_bytes=64)
        w_in_hbm = w_qkv_words[0].rearrange("p (w c) -> p w c", w=3)
        nc.sync.dma_start(
            out=w_words[:, Q : V + 1 : 2, :].bitcast(I32),
            in_=w_in_hbm[:, Q : V + 1 : 2, :].bitcast(I32),
        )
        w_scales = keep.tile([P, 3 * MODEL], U8, align_bytes=64)
        nc.vector.memset(w_scales[:].bitcast(I32), 0)
        for quadrant in range(4):
            nc.sync.dma_start(
                out=w_scales[32 * quadrant : 32 * quadrant + 4, :].bitcast(I32),
                in_=w_qkv_scales[0, 4 * quadrant : 4 * quadrant + 4, :].bitcast(I32),
            )
        nc.sync.dma_start(
            out=w_words[:, K, :].bitcast(I32), in_=w_in_hbm[:, K, :].bitcast(I32)
        )

        zeros = keep.tile([P, P], F32)
        nc.gpsimd.memset(zeros[:], 0.0)
        for warm in range(WARM_UP):
            unused = new_tile_in_bank(warm, [P])
            nc.tensor.matmul(unused[:], lhsT=zeros[:], rhs=zeros[:], start=True, stop=True)

        identity = keep.tile([P, P], F32)
        make_identity(nc, identity[:])
        exchange = keep.tile([P, PAIRS * 2, 2], F32)
        by_pair = identity[:].rearrange("p (c u) -> p c u", u=2)
        for u in range(2):
            nc.gpsimd.tensor_copy(out=exchange[:, :, u], in_=by_pair[:, :, 1 - u])

        spread = keep.tile([P, 2, PARITY, 2, PAIRS, 2], F32)
        cos_spread, sin_spread = [
            table_sb[:]
            .rearrange("p (e j) -> p e j", e=PARITY)
            .unsqueeze(2)
            .to_broadcast([P, PARITY, 2, PAIRS])
            for table_sb in (cos_sb, sin_sb)
        ]
        nc.scalar.copy(out=spread[:, 1, :, :, :, 0], in_=sin_spread)
        nc.gpsimd.tensor_scalar(
            out=spread[:, 1, :, :, :, 1], in0=sin_spread, scalar1=-1.0, scalar2=0.0, op0=MULT, op1=ADD
        )
        nc.vector.tensor_copy(
            out=spread[:, 0],
            in_=cos_spread.unsqueeze(4).to_broadcast([P, PARITY, 2, PAIRS, 2]),
        )
        factors = keep.tile([P, PARITY * PAIRS, 4], BF16)
        factors_by_e = factors[:].rearrange("p (e j) (a u) -> p e j a u", e=PARITY, u=2)

        x_as_words = x_sb[:].bitcast(F32)
        words_per_row = MODEL // 2
        grouped = []
        for e in range(PARITY):
            grouped_e = keep.tile([P, P, PACK], BF16, align_bytes=64, name="grouped%d" % e)
            grouped.append(grouped_e)
            flipped = new_tile_in_bank(4 + e, [2, P])
            for u in range(2):
                nc.tensor.transpose(
                    flipped[:, u, :],
                    x_as_words[:, words_per_row * e + u : words_per_row * (e + 1) : 2],
                    identity[:],
                )
            copier = nc.vector.tensor_copy if e == 0 else nc.scalar.copy
            copier(out=grouped_e[:].bitcast(F32), in_=flipped[:].rearrange("p u m -> p m u"))
        nc.vector.tensor_copy(out=factors[:, :, 2], in_=sin_sb[:])
        table_bank = new_tile_in_bank(6, [2, PARITY, P])
        for w in range(2):
            for e in range(PARITY):
                nc.tensor.transpose(
                    table_bank[:, w, e, :],
                    spread[:, w, e].rearrange("p g j u -> p (g j u)"),
                    identity[:],
                )
        tables_t = keep.tile([P, 2, 2, P // 2, BATCH], BF16)
        for w in range(2):
            nc.scalar.copy(
                out=tables_t[:, w],
                in_=table_bank[:, w].rearrange("p e (i r b) -> p r (e i) b", r=2, b=BATCH),
            )
        x_codes = keep.tile([P, PARITY * P], U32, align_bytes=64)
        x_scales = keep.tile([P, PARITY * P], U8, align_bytes=64)

        def quantise(e):
            nc.vector.quantize_mx(
                out=x_codes[:, P * e : P * (e + 1)].bitcast(FP8X4),
                scales=x_scales[:, P * e : P * (e + 1)],
                in_=grouped[e][:].rearrange("p m t -> p (m t)"),
            )

        quantise(0)
        nc.vector.tensor_scalar_mul(out=factors[:, :, 1], in0=sin_sb[:], scalar1=-1.0)
        nc.vector.tensor_copy(
            out=factors[:, :, 0:4:3],
            in_=cos_sb[:].unsqueeze(2).to_broadcast([P, PARITY * PAIRS, 2]),
        )
        quantise(1)

        def project(unit, e, acc, half=0):
            which, first_head = unit
            head_col = first_head * HEAD_DIM
            first_col = which * MODEL + head_col
            nc.tensor.matmul_mx(
                out=acc[:, half, :],
                lhsT=x_codes[:, P * e : P * (e + 1)].bitcast(FP8X4),
                lhsT_scale=x_scales[:, P * e : P * (e + 1)],
                rhs=w_words[:, which, 2 * head_col : 2 * (head_col + UNIT_COLS)].bitcast(FP4X4),
                rhs_scale=w_scales[:, first_col : first_col + UNIT_COLS],
                start=True,
                stop=True,
            )
            return acc

        def store(queues, which, first_head, result):
            heads = result[:].shape[1]
            for b in range(BATCH):
                queues[b].dma_start(
                    out=outputs[which][b, first_head : first_head + heads].rearrange(
                        "h (i e) d -> i h (e d)", e=PARITY
                    ),
                    in_=result[b:P:BATCH].rearrange("p h e d -> p h (e d)"),
                )

        def new_products():
            products = work.tile([P, UNIT_HEADS, PARITY, 2 * HEAD_DIM], F32, tag="products")
            return products

        def multiply(engine, sums, e, products):
            heads = products.shape[1]
            shape = [P, heads, PAIRS, 2, 2]
            engine.tensor_tensor(
                out=products[:, :, e, :].rearrange("p h (j a u) -> p h j a u", a=2, u=2),
                in0=sums.rearrange("p (h j u) -> p h j u", h=heads, u=2)
                .unsqueeze(3)
                .to_broadcast(shape),
                in1=factors_by_e[:, e].unsqueeze(1).to_broadcast(shape),
                op=MULT,
            )

        def add_parity(engine, products, e, rotated):
            both_terms = products[:, :, e, :].rearrange("p h (c u) -> p h c u", u=2)
            engine.tensor_tensor(
                out=rotated[:, :, e, :],
                in0=both_terms[:, :, :, 0],
                in1=both_terms[:, :, :, 1],
                op=ADD,
            )

        def new_result(heads):
            rotated = results.tile([P, heads, PARITY, HEAD_DIM], F32, tag="result")
            return rotated

        def copy_out_in_halves(accs):
            halves = [new_result(2), new_result(2)]
            for e in range(PARITY):
                heads = accs[e][:, 0, :].rearrange("p (h d) -> p h d", h=UNIT_HEADS)
                for part, copied in enumerate(halves):
                    nc.scalar.copy(out=copied[:, :, e, :], in_=heads[:, 2 * part : 2 * part + 2])
            return halves

        def copy_out_bank(bank):
            copied = results.tile([P, UNIT_HEADS, PARITY, HEAD_DIM], F32, tag="result")
            nc.scalar.copy(
                out=copied[:].rearrange("p h e d -> p e h d"),
                in_=bank[:].rearrange("p e (h d) -> p e h d", h=UNIT_HEADS),
            )
            return copied

        def project_turned(unit, acc):
            which, first_head = unit
            head_col = first_head * HEAD_DIM
            first_col = which * MODEL + head_col
            for pair in range(2):
                nc.tensor.matmul_mx(
                    out=acc[:, pair, :],
                    lhsT=w_words[:, which, 2 * (head_col + P * pair) : 2 * (head_col + P * (pair + 1))].bitcast(FP4X4),
                    lhsT_scale=w_scales[:, first_col + P * pair : first_col + P * (pair + 1)],
                    rhs=x_codes[:].bitcast(FP8X4),
                    rhs_scale=x_scales[:],
                    start=True,
                    stop=True,
                )
            return acc

        def multiply_turned(acc):
            sums = acc[:].rearrange("p g (e i r b) -> p r (e i) g b", e=PARITY, r=2, b=BATCH)
            products = []
            for r in range(2):
                prod_t = work.tile([P, 2, P // 2, 2, BATCH], F32, tag="prod_t")
                for w in range(2):
                    parts = PARITY if r and w else 1
                    part = P // 2 // parts
                    for first in range(0, P // 2, part):
                        nc.vector.tensor_tensor(
                            out=prod_t[:, w, first : first + part],
                            in0=sums[:, r, first : first + part],
                            in1=tables_t[:, w, r, first : first + part]
                            .unsqueeze(2)
                            .to_broadcast([P, part, 2, BATCH]),
                            op=MULT,
                        )
                products.append(prod_t)
            return products

        def turn_back(products, rotated):
            for r in range(2):
                columns = products[r][:].rearrange("p w (e i) g b -> p w e (i g b)", e=PARITY)
                summed = []
                for e in both:
                    summed.append(new_tile_in_bank(2 * r + e, [2, HEAD_DIM]))
                for w, order in ((0, identity[:]), (1, exchange[:].rearrange("p c u -> p (c u)"))):
                    for e in both:
                        nc.tensor.matmul(
                            summed[e][:].rearrange("p g d -> p (g d)"),
                            lhsT=columns[:, w, e],
                            rhs=order,
                            start=w == 0,
                            stop=w == 1,
                            is_transpose=True,
                        )
                for e in both:
                    nc.scalar.copy(out=rotated[:, :, r, e], in_=summed[e][:])

        def store_turned(which, first_head, rotated):
            for b in range(BATCH):
                nc.sync.dma_start(
                    out=outputs[which][b, first_head : first_head + UNIT_HEADS].rearrange(
                        "h (i t) d -> i h (t d)", t=2 * PARITY
                    ),
                    in_=rotated[b:P:BATCH].rearrange("p g r e d -> p g (r e d)"),
                )

        def new_turned():
            rotated = results.tile([P, 2, 2, PARITY, HEAD_DIM], F32, tag="turned")
            return rotated

        both = range(PARITY)
        q0, q4, k0, k4, v0, v4 = (Q, 0), (Q, 4), (K, 0), (K, 4), (V, 0), (V, 4)

        sync2 = (nc.sync, nc.sync)
        sums_shape = [PARITY, UNIT_COLS]
        acc_q0 = [new_tile_in_bank(bank, sums_shape) for bank in (7, 2)]
        acc_v0 = [new_tile_in_bank(bank, sums_shape) for bank in (0, 3)]
        bank_v4 = new_tile_in_bank(1, sums_shape)
        project(q0, 0, acc_q0[0])
        project(v0, 0, acc_v0[0])
        project(v4, 0, bank_v4, 0)
        project(v0, 1, acc_v0[1])
        project(q0, 1, acc_q0[1])
        project(v4, 1, bank_v4, 1)
        acc_q4 = project_turned(q4, new_tile_in_bank(4, sums_shape))
        acc_k0 = project_turned(k0, new_tile_in_bank(5, sums_shape))
        acc_k4 = [project(k4, e, new_tile_in_bank(6 + e, sums_shape)) for e in both]

        prod_q0 = new_products()
        for e in both:
            multiply(nc.vector, acc_q0[e][:, 0, :], e, prod_q0[:])
        for part, half in enumerate(copy_out_in_halves(acc_v0)):
            store(sync2, V, 2 * part, half)
        store(sync2, V, 4, copy_out_bank(bank_v4))
        sums_k4 = keep.tile([P, POOL_HEADS * HEAD_DIM], F32)
        nc.scalar.copy(out=sums_k4[:], in_=acc_k4[0][:, 0, 0 : POOL_HEADS * HEAD_DIM])
        rot_q0 = new_result(4)
        for e in both:
            add_parity(nc.gpsimd, prod_q0, e, rot_q0)
        store(sync2, Q, 0, rot_q0)

        rot_q4 = new_turned()
        turn_back(multiply_turned(acc_q4), rot_q4)
        store_turned(Q, 4, rot_q4)

        prod_k4 = new_products()
        multiply(nc.gpsimd, sums_k4[:], 0, prod_k4[:, 0:POOL_HEADS])
        rot_k0 = new_turned()
        turn_back(multiply_turned(acc_k0), rot_k0)

        multiply(
            nc.vector, acc_k4[0][:, 0, POOL_HEADS * HEAD_DIM :], 0, prod_k4[:, POOL_HEADS:]
        )
        rot_k4 = new_result(4)
        pairs_of_heads = (slice(0, 2), slice(2, 4))
        sums_k4_odd = acc_k4[1][:, 0, :].rearrange("p (g c) -> p g c", g=2)
        for g, heads in enumerate(pairs_of_heads):
            multiply(nc.vector, sums_k4_odd[:, g], 1, prod_k4[:, heads])
        add_parity(nc.vector, prod_k4, 0, rot_k4)
        for heads in pairs_of_heads:
            add_parity(nc.vector, prod_k4[:, heads], 1, rot_k4[:, heads])
        store_turned(K, 0, rot_k0)
        store(sync2, K, 4, rot_k4)
